import numpy as np
import ml_dtypes


def mxq(x, axis, fmt="e4m3"):
    dtype, down = {"e4m3": (ml_dtypes.float8_e4m3fn, 7), "e5m2": (ml_dtypes.float8_e5m2, 14)}[fmt]
    v = np.moveaxis(np.asarray(x, np.float32).astype(ml_dtypes.bfloat16).astype(np.float64), axis, -1)
    blocks = v.reshape(v.shape[:-1] + (-1, 32))
    amax = np.abs(blocks).max(-1, keepdims=True)
    byte = np.maximum(np.where(amax > 0, np.frexp(amax)[1] - 1 + 127, 0) - down, 1)
    scale = np.exp2(byte - 127.0)
    codes = (blocks / scale).astype(np.float32).astype(dtype).astype(np.float64)
    return np.moveaxis((codes * scale).reshape(v.shape), -1, axis)


WIDE = False


def mx_kscale(k):
    if not WIDE:
        return np.ones(k)
    levels = np.array([10, -10, 5, -5, 0])
    a = np.random.permutation(np.resize(levels, k // 512 * 4)).reshape(k // 512, 4)
    idx = np.arange(k)
    return np.exp2(a[idx // 512, idx % 128 // 32])


BF16 = ml_dtypes.bfloat16


def bf(x):
    return np.asarray(x, np.float32).astype(BF16)


def f64(x):
    return np.asarray(x).astype(np.float64)


B, T, D = 8, 512, 512


def sigmoid(v):
    return 1.0 / (1.0 + np.exp(-v))


def setup_inputs():
    s = mx_kscale(D)
    t = np.exp2(np.round(np.log2(mx_kscale(D)) / 2))
    w = 1.2 / np.sqrt(D)
    wo = 1.6 / np.sqrt(D)
    return {"x": bf(np.random.standard_normal((B, T, D)) * s),
            "state": bf(np.random.standard_normal((B, T, D)) * t),
            "Wk": bf(np.random.standard_normal((D, D)) * w / s[None, :]),
            "Wv": bf(np.random.standard_normal((D, D)) * w / s[None, :] * t[:, None]),
            "Wr": bf(np.random.standard_normal((D, D)) * w / s[None, :]),
            "Wo": bf(np.random.standard_normal((D, D)) * wo / t[None, :]),
            "time_decay": bf(np.random.uniform(-3.0, 1.0, D)),
            "time_curve": bf(np.random.uniform(0.0, 1.0, D))}


def reference(x, state, Wk, Wv, Wr, Wo, time_decay, time_curve):
    x = f64(x)
    tc = f64(time_curve)
    xx = np.concatenate([np.zeros_like(x[:, :1]), x[:, :-1]], axis=1)
    xm = x * tc + xx * (1.0 - tc)
    xq = mxq(xm, 2, "e4m3")
    k = xq @ mxq(f64(Wk), 1, "e4m3").T
    v = xq @ mxq(f64(Wv), 1, "e4m3").T
    r = xq @ mxq(f64(Wr), 1, "e4m3").T
    sr = sigmoid(r)
    decay = np.exp(-np.exp(f64(time_decay)))
    new_state = k * v + decay * f64(state)
    out = mxq(sr * new_state, 2, "e4m3") @ mxq(f64(Wo), 1, "e4m3").T
    return out, new_state

@@ -1,0 +1,287 @@
+from contextlib import ExitStack
+
+import concourse.mybir as mybir
+from concourse.masks import make_identity
+
+F32 = mybir.dt.float32
+BF16 = mybir.dt.bfloat16
+U32 = mybir.dt.uint32
+U8 = mybir.dt.uint8
+FP8X4 = mybir.dt.float8_e4m3fn_x4
+ACT = mybir.ActivationFunctionType
+ALU = mybir.AluOpType
+
+P = 128
+PACK = 4
+SEQS = 8
+T = 512
+D = 512
+N_WEIGHTS = 4
+K_W, V_W, R_W, O_W = 0, 1, 2, 3
+
+FLOPS = 2 * N_WEIGHTS * SEQS * T * D * D
+
+STEPS = SEQS * PACK
+HIDDEN_LAG = PACK
+QUANTISE_LAG = PACK + 1
+STATE_OUT_LAG = PACK + 1
+PROJECT_LAG = PACK + 2
+
+
+def block(i):
+    return slice(i * P, (i + 1) * P)
+
+
+def tile_rwkvtimemix_pa_t_kernel(
+    tc, x, state, Wk, Wv, Wr, Wo, time_decay, time_curve, out_0, out_1
+):
+    nc = tc.nc
+    weights = (Wk, Wv, Wr, Wo)
+
+    with ExitStack() as stack:
+        stack.enter_context(tc.manual_schedule())
+        keep = stack.enter_context(tc.tile_pool(name="keep", bufs=1))
+        pairs = stack.enter_context(tc.tile_pool(name="pairs", bufs=2))
+        triples = stack.enter_context(tc.tile_pool(name="triples", bufs=3))
+        stores = stack.enter_context(tc.tile_pool(name="stores", bufs=4))
+
+        w_rows = [keep.tile([P, PACK, D], BF16, name="w_rows%d" % w) for w in range(N_WEIGHTS)]
+        x_rows = [keep.tile([P, PACK, D], BF16, name="x_rows%d" % s) for s in range(SEQS)]
+        state_rows = [keep.tile([P, PACK, D], BF16, name="state_rows%d" % s) for s in range(SEQS)]
+
+        vec_rows = keep.tile([P, P], BF16, name="vec_rows")
+        nc.vector.memset(vec_rows[:], 0.0)
+        nc.scalar.dma_start(
+            out=vec_rows[0:PACK, :], in_=time_decay.rearrange("(j p) -> j p", p=P)
+        )
+        nc.scalar.dma_start(
+            out=vec_rows[PACK : 2 * PACK, :], in_=time_curve.rearrange("(j p) -> j p", p=P)
+        )
+        for w in range(N_WEIGHTS):
+            nc.sync.dma_start(out=w_rows[w][:], in_=weights[w].rearrange("(a p) c -> p a c", p=P))
+        for s in range(SEQS):
+            nc.sync.dma_start(out=x_rows[s][:], in_=x[s].rearrange("(a p) c -> p a c", p=P))
+        for s in range(SEQS):
+            nc.sync.dma_start(
+                out=state_rows[s][:], in_=state[s].rearrange("(a p) c -> p a c", p=P)
+            )
+
+        ident_bf16 = keep.tile([P, P], BF16, name="ident_bf16")
+        make_identity(nc, ident_bf16[:])
+        ident_f32 = keep.tile([P, P], F32, name="ident_f32")
+        make_identity(nc, ident_f32[:])
+
+        w_codes = [
+            keep.tile([P, D], U32, name="w_codes%d" % w, align_bytes=64) for w in range(N_WEIGHTS)
+        ]
+        w_scales = [
+            keep.tile([P, D], U8, name="w_scales%d" % w, align_bytes=64) for w in range(N_WEIGHTS)
+        ]
+        xm_codes = keep.tile([P, SEQS, T], U32, name="xm_codes", align_bytes=64)
+        xm_scales = keep.tile([P, SEQS, T], U8, name="xm_scales", align_bytes=64)
+
+        shifted = [keep.tile([P, T], F32, name="shifted%d" % i) for i in range(PACK)]
+        for tile_ in shifted:
+            nc.vector.memset(tile_[:], 0.0)
+
+        with tc.psum_pool(name="vec_bank", bufs=1, reuse_waits="tile") as vec_bank, tc.psum_pool(
+            name="w_banks", bufs=2, reuse_waits="tile"
+        ) as w_banks, tc.psum_pool(name="x_banks", bufs=4, reuse_waits="tile") as x_banks:
+            vec_cols = vec_bank.tile([P, P], BF16, name="vec_cols")
+            nc.tensor.transpose(vec_cols[:], vec_rows[:], ident_bf16[:])
+            per_channel = keep.tile([P, 2 * PACK], F32, name="per_channel")
+            nc.vector.tensor_copy(out=per_channel[:], in_=vec_cols[:, 0 : 2 * PACK])
+            curve = per_channel[:, PACK : 2 * PACK]
+            one_minus_curve = keep.tile([P, PACK], F32, name="one_minus_curve")
+            nc.vector.tensor_scalar(
+                out=one_minus_curve[:], in0=curve, scalar1=-1.0, scalar2=1.0,
+                op0=ALU.mult, op1=ALU.add,
+            )
+            rate = keep.tile([P, PACK], F32, name="rate")
+            nc.scalar.activation(out=rate[:], in_=per_channel[:, 0:PACK], func=ACT.Exp)
+            decay = keep.tile([P, PACK], F32, name="decay")
+            nc.scalar.activation(out=decay[:], in_=rate[:], func=ACT.Exp, scale=-1.0)
+
+            w_grouped = {}
+
+            def turn_weight(w):
+                w_grouped[w] = pairs.tile([P, D, PACK], BF16, name="w_grouped", align_bytes=64)
+                for half in range(2):
+                    w_cols = w_banks.tile([P, 2, PACK, P], BF16, name="w_cols")
+                    for b in range(2):
+                        for j in range(PACK):
+                            nc.tensor.transpose(
+                                w_cols[:, b, j, :], w_rows[w][:, 2 * half + b, block(j)],
+                                ident_bf16[:],
+                            )
+                    copy = nc.vector.tensor_copy if half == 0 else nc.scalar.copy
+                    copy(
+                        out=w_grouped[w][:, 2 * half * P : 2 * (half + 1) * P, :].rearrange(
+                            "p (b o) j -> p b o j", b=2
+                        ),
+                        in_=w_cols[:].rearrange("p b j o -> p b o j"),
+                    )
+
+            def quantise_weight(w):
+                nc.vector.quantize_mx(
+                    out=w_codes[w][:].bitcast(FP8X4),
+                    scales=w_scales[w][:],
+                    in_=w_grouped[w][:].rearrange("p o j -> p (o j)"),
+                )
+
+            for w in range(N_WEIGHTS):
+                turn_weight(w)
+                if w > 0:
+                    quantise_weight(w - 1)
+            quantise_weight(N_WEIGHTS - 1)
+
+            xm_grouped = {}
+
+            def mix(s):
+                xm_planes = pairs.tile([P, PACK, T], BF16, name="xm_planes")
+                for j in range(PACK):
+                    x_cols = x_banks.tile([P, T], BF16, name="x_cols")
+                    for a in range(PACK):
+                        nc.tensor.transpose(
+                            x_cols[:, block(a)], x_rows[s][:, a, block(j)], ident_bf16[:]
+                        )
+                    before = shifted[j]
+                    nc.scalar.activation(
+                        out=before[:, 1:T], in_=x_cols[:, 0 : T - 1], func=ACT.Copy,
+                        scale=one_minus_curve[:, j : j + 1],
+                    )
+                    nc.vector.scalar_tensor_tensor(
+                        out=xm_planes[:, j, :], in0=x_cols[:], scalar=curve[:, j : j + 1],
+                        in1=before[:], op0=ALU.mult, op1=ALU.add,
+                    )
+                xm_grouped[s] = pairs.tile([P, T, PACK], BF16, name="xm_grouped", align_bytes=64)
+                nc.vector.tensor_copy(
+                    out=xm_grouped[s][:].rearrange("p (c i) j -> p c j i", i=4),
+                    in_=xm_planes[:].rearrange("p j (c i) -> p c j i", i=4),
+                )
+
+            def quantise_mix(s):
+                nc.vector.quantize_mx(
+                    out=xm_codes[:, s, :].bitcast(FP8X4),
+                    scales=xm_scales[:, s, :],
+                    in_=xm_grouped[s][:].rearrange("p t j -> p (t j)"),
+                )
+
+            for s in range(SEQS):
+                mix(s)
+                if s > 0:
+                    quantise_mix(s - 1)
+            quantise_mix(SEQS - 1)
+
+        with tc.psum_pool(name="gate_banks", bufs=1, reuse_waits="tile") as gate_banks, tc.psum_pool(
+            name="state_banks", bufs=2, reuse_waits="tile"
+        ) as state_banks, tc.psum_pool(name="token_banks", bufs=3, reuse_waits="tile") as token_banks:
+            state_cols = {}
+            gate = {}
+            new_state = {}
+            h_grouped = {}
+            h_codes = {}
+            h_scales = {}
+
+            def turn_state(step):
+                s, m = divmod(step, PACK)
+                state_cols[step] = state_banks.tile([P, T], BF16, name="state_cols")
+                for a in range(PACK):
+                    nc.tensor.transpose(
+                        state_cols[step][:, block(a)], state_rows[s][:, a, block(m)], ident_bf16[:]
+                    )
+
+            def product(bank, w, s, m):
+                nc.tensor.matmul_mx(
+                    out=bank[:],
+                    lhsT=w_codes[w][:, block(m)].bitcast(FP8X4),
+                    lhsT_scale=w_scales[w][:, block(m)],
+                    rhs=xm_codes[:, s, :].bitcast(FP8X4),
+                    rhs_scale=xm_scales[:, s, :],
+                    start=True,
+                    stop=True,
+                )
+
+            def gates(step):
+                s, m = divmod(step, PACK)
+                if m == 0:
+                    gate[s] = pairs.tile([P, PACK, T], F32, name="gate")
+                    new_state[s] = triples.tile([P, PACK, T], F32, name="new_state")
+                v_bank = gate_banks.tile([P, T], F32, name="v_bank")
+                product(v_bank, V_W, s, m)
+                r_bank = gate_banks.tile([P, T], F32, name="r_bank")
+                product(r_bank, R_W, s, m)
+                k_bank = gate_banks.tile([P, T], F32, name="k_bank")
+                product(k_bank, K_W, s, m)
+                v_copy = triples.tile([P, T], F32, name="v_copy")
+                nc.scalar.copy(out=v_copy[:], in_=v_bank[:])
+                nc.scalar.activation(out=gate[s][:, m, :], in_=r_bank[:], func=ACT.Sigmoid)
+                kv = triples.tile([P, T], F32, name="kv")
+                nc.vector.tensor_tensor(out=kv[:], in0=k_bank[:], in1=v_copy[:], op=ALU.mult)
+                nc.vector.scalar_tensor_tensor(
+                    out=new_state[s][:, m, :], in0=state_cols[step][:],
+                    scalar=decay[:, m : m + 1], in1=kv[:], op0=ALU.mult, op1=ALU.add,
+                )
+
+            def hidden(step):
+                s, a = divmod(step, PACK)
+                h_grouped[step] = triples.tile([P, P, PACK], BF16, name="h_grouped", align_bytes=64)
+                nc.vector.tensor_tensor(
+                    out=h_grouped[step][:],
+                    in0=gate[s][:, :, block(a)].rearrange("p m t -> p t m"),
+                    in1=new_state[s][:, :, block(a)].rearrange("p m t -> p t m"),
+                    op=ALU.mult,
+                )
+
+            def quantise_hidden(step):
+                h_codes[step] = triples.tile([P, P], U32, name="h_codes", align_bytes=64)
+                h_scales[step] = triples.tile([P, P], U8, name="h_scales", align_bytes=64)
+                nc.vector.quantize_mx(
+                    out=h_codes[step][:].bitcast(FP8X4),
+                    scales=h_scales[step][:],
+                    in_=h_grouped[step][:].rearrange("p t m -> p (t m)"),
+                )
+
+            def return_state(step):
+                s, a = divmod(step, PACK)
+                state_bank = token_banks.tile([P, D], F32, name="token_bank")
+                for m in range(PACK):
+                    nc.tensor.transpose(
+                        state_bank[:, block(m)], new_state[s][:, m, block(a)], ident_f32[:]
+                    )
+                state_out = stores.tile([P, D], F32, name="state_out")
+                nc.scalar.copy(out=state_out[:], in_=state_bank[:])
+                nc.sync.dma_start(out=out_1[s, block(a), :], in_=state_out[:])
+
+            def project(step):
+                s, a = divmod(step, PACK)
+                out_bank = token_banks.tile([P, D], F32, name="token_bank")
+                nc.tensor.matmul_mx(
+                    out=out_bank[:],
+                    lhsT=h_codes[step][:].bitcast(FP8X4),
+                    lhsT_scale=h_scales[step][:],
+                    rhs=w_codes[O_W][:].bitcast(FP8X4),
+                    rhs_scale=w_scales[O_W][:],
+                    start=True,
+                    stop=True,
+                )
+                out_rows = stores.tile([P, D], F32, name="out_rows")
+                nc.scalar.copy(out=out_rows[:], in_=out_bank[:])
+                nc.sync.dma_start(out=out_0[s, block(a), :], in_=out_rows[:])
+
+            def due(step, lag):
+                return 0 <= step - lag < STEPS
+
+            for step in range(STEPS + PROJECT_LAG):
+                if due(step, 0):
+                    turn_state(step)
+                if due(step, STATE_OUT_LAG):
+                    return_state(step - STATE_OUT_LAG)
+                if due(step, 0):
+                    gates(step)
+                if due(step, QUANTISE_LAG):
+                    quantise_hidden(step - QUANTISE_LAG)
+                if due(step, HIDDEN_LAG):
+                    hidden(step - HIDDEN_LAG)
+                if due(step, PROJECT_LAG):
+                    project(step - PROJECT_LAG)

@@ -18,18 +18,24 @@ T = 512
 D = 512
 N_WEIGHTS = 4
 K_W, V_W, R_W, O_W = 0, 1, 2, 3
+LATER_WEIGHTS = (V_W, K_W, O_W)
 
 FLOPS = 2 * N_WEIGHTS * SEQS * T * D * D
 
 STEPS = SEQS * PACK
+GATE_LAG = PACK + 2
 HIDDEN_LAG = PACK
 QUANTISE_LAG = PACK + 1
 STATE_OUT_LAG = PACK + 1
-PROJECT_LAG = PACK + 2
+PROJECT_LAG = PACK + 3
 
 
 def block(i):
     return slice(i * P, (i + 1) * P)
+
+
+def due(step, lag):
+    return 0 <= step - lag < STEPS
 
 
 def tile_rwkvtimemix_pa_t_kernel(
@@ -41,30 +47,16 @@ def tile_rwkvtimemix_pa_t_kernel(
     with ExitStack() as stack:
         stack.enter_context(tc.manual_schedule())
         keep = stack.enter_context(tc.tile_pool(name="keep", bufs=1))
-        pairs = stack.enter_context(tc.tile_pool(name="pairs", bufs=2))
-        triples = stack.enter_context(tc.tile_pool(name="triples", bufs=3))
-        stores = stack.enter_context(tc.tile_pool(name="stores", bufs=4))
 
-        w_rows = [keep.tile([P, PACK, D], BF16, name="w_rows%d" % w) for w in range(N_WEIGHTS)]
-        x_rows = [keep.tile([P, PACK, D], BF16, name="x_rows%d" % s) for s in range(SEQS)]
-        state_rows = [keep.tile([P, PACK, D], BF16, name="state_rows%d" % s) for s in range(SEQS)]
+        def load_rows(rows, matrix):
+            nc.sync.dma_start(out=rows[:], in_=matrix.rearrange("(a p) c -> p a c", p=P))
 
         vec_rows = keep.tile([P, P], BF16, name="vec_rows")
         nc.vector.memset(vec_rows[:], 0.0)
-        nc.scalar.dma_start(
-            out=vec_rows[0:PACK, :], in_=time_decay.rearrange("(j p) -> j p", p=P)
-        )
-        nc.scalar.dma_start(
+        nc.sync.dma_start(out=vec_rows[0:PACK, :], in_=time_decay.rearrange("(j p) -> j p", p=P))
+        nc.sync.dma_start(
             out=vec_rows[PACK : 2 * PACK, :], in_=time_curve.rearrange("(j p) -> j p", p=P)
         )
-        for w in range(N_WEIGHTS):
-            nc.sync.dma_start(out=w_rows[w][:], in_=weights[w].rearrange("(a p) c -> p a c", p=P))
-        for s in range(SEQS):
-            nc.sync.dma_start(out=x_rows[s][:], in_=x[s].rearrange("(a p) c -> p a c", p=P))
-        for s in range(SEQS):
-            nc.sync.dma_start(
-                out=state_rows[s][:], in_=state[s].rearrange("(a p) c -> p a c", p=P)
-            )
 
         ident_bf16 = keep.tile([P, P], BF16, name="ident_bf16")
         make_identity(nc, ident_bf16[:])
@@ -80,26 +72,55 @@ def tile_rwkvtimemix_pa_t_kernel(
         xm_codes = keep.tile([P, SEQS, T], U32, name="xm_codes", align_bytes=64)
         xm_scales = keep.tile([P, SEQS, T], U8, name="xm_scales", align_bytes=64)
 
-        shifted = [keep.tile([P, T], F32, name="shifted%d" % i) for i in range(PACK)]
-        for tile_ in shifted:
-            nc.vector.memset(tile_[:], 0.0)
+        state_rows = [keep.tile([P, PACK, D], BF16, name="state_rows%d" % s) for s in range(SEQS)]
+        gate = keep.tile([P, SEQS, PACK, T], F32, name="gate")
+        decay = keep.tile([P, PACK], F32, name="decay")
 
-        with tc.psum_pool(name="vec_bank", bufs=1, reuse_waits="tile") as vec_bank, tc.psum_pool(
-            name="w_banks", bufs=2, reuse_waits="tile"
-        ) as w_banks, tc.psum_pool(name="x_banks", bufs=4, reuse_waits="tile") as x_banks:
+        def product(bank, w, s, m):
+            nc.tensor.matmul_mx(
+                out=bank[:],
+                lhsT=w_codes[w][:, block(m)].bitcast(FP8X4),
+                lhsT_scale=w_scales[w][:, block(m)],
+                rhs=xm_codes[:, s, :].bitcast(FP8X4),
+                rhs_scale=xm_scales[:, s, :],
+                start=True,
+                stop=True,
+            )
+
+        with ExitStack() as part:
+            rows = part.enter_context(tc.tile_pool(name="rows", bufs=1))
+            pairs = part.enter_context(tc.tile_pool(name="pairs", bufs=2))
+            vec_bank = part.enter_context(tc.psum_pool(name="vec_bank", bufs=1))
+            w_banks = part.enter_context(tc.psum_pool(name="w_banks", bufs=2))
+            x_banks = part.enter_context(tc.psum_pool(name="x_banks", bufs=3))
+            r_banks = part.enter_context(tc.psum_pool(name="r_banks", bufs=2))
+
+            w_rows = [rows.tile([P, PACK, D], BF16, name="w_rows%d" % w) for w in range(N_WEIGHTS)]
+            x_rows = [rows.tile([P, PACK, D], BF16, name="x_rows%d" % s) for s in range(SEQS)]
+            load_rows(w_rows[R_W], weights[R_W])
+            for s in range(SEQS):
+                load_rows(x_rows[s], x[s])
+                if s < len(LATER_WEIGHTS):
+                    load_rows(w_rows[LATER_WEIGHTS[s]], weights[LATER_WEIGHTS[s]])
+            for s in range(SEQS):
+                load_rows(state_rows[s], state[s])
+
+            shifted = [rows.tile([P, T], F32, name="shifted%d" % j) for j in range(PACK)]
+            for j in range(PACK):
+                nc.vector.memset(shifted[j][:], 0.0)
+
             vec_cols = vec_bank.tile([P, P], BF16, name="vec_cols")
             nc.tensor.transpose(vec_cols[:], vec_rows[:], ident_bf16[:])
-            per_channel = keep.tile([P, 2 * PACK], F32, name="per_channel")
+            per_channel = rows.tile([P, 2 * PACK], F32, name="per_channel")
             nc.vector.tensor_copy(out=per_channel[:], in_=vec_cols[:, 0 : 2 * PACK])
             curve = per_channel[:, PACK : 2 * PACK]
-            one_minus_curve = keep.tile([P, PACK], F32, name="one_minus_curve")
+            one_minus_curve = rows.tile([P, PACK], F32, name="one_minus_curve")
             nc.vector.tensor_scalar(
                 out=one_minus_curve[:], in0=curve, scalar1=-1.0, scalar2=1.0,
                 op0=ALU.mult, op1=ALU.add,
             )
-            rate = keep.tile([P, PACK], F32, name="rate")
+            rate = rows.tile([P, PACK], F32, name="rate")
             nc.scalar.activation(out=rate[:], in_=per_channel[:, 0:PACK], func=ACT.Exp)
-            decay = keep.tile([P, PACK], F32, name="decay")
             nc.scalar.activation(out=decay[:], in_=rate[:], func=ACT.Exp, scale=-1.0)
 
             w_grouped = {}
@@ -114,8 +135,7 @@ def tile_rwkvtimemix_pa_t_kernel(
                                 w_cols[:, b, j, :], w_rows[w][:, 2 * half + b, block(j)],
                                 ident_bf16[:],
                             )
-                    copy = nc.vector.tensor_copy if half == 0 else nc.scalar.copy
-                    copy(
+                    nc.vector.tensor_copy(
                         out=w_grouped[w][:, 2 * half * P : 2 * (half + 1) * P, :].rearrange(
                             "p (b o) j -> p b o j", b=2
                         ),
@@ -129,35 +149,31 @@ def tile_rwkvtimemix_pa_t_kernel(
                     in_=w_grouped[w][:].rearrange("p o j -> p (o j)"),
                 )
 
-            for w in range(N_WEIGHTS):
-                turn_weight(w)
-                if w > 0:
-                    quantise_weight(w - 1)
-            quantise_weight(N_WEIGHTS - 1)
-
+            xm_planes = {}
             xm_grouped = {}
 
-            def mix(s):
-                xm_planes = pairs.tile([P, PACK, T], BF16, name="xm_planes")
-                for j in range(PACK):
-                    x_cols = x_banks.tile([P, T], BF16, name="x_cols")
-                    for a in range(PACK):
-                        nc.tensor.transpose(
-                            x_cols[:, block(a)], x_rows[s][:, a, block(j)], ident_bf16[:]
-                        )
-                    before = shifted[j]
-                    nc.scalar.activation(
-                        out=before[:, 1:T], in_=x_cols[:, 0 : T - 1], func=ACT.Copy,
-                        scale=one_minus_curve[:, j : j + 1],
+            def mix_plane(s, j):
+                if j == 0:
+                    xm_planes[s] = pairs.tile([P, PACK, T], BF16, name="xm_planes")
+                x_cols = x_banks.tile([P, T], BF16, name="x_cols")
+                for a in range(PACK):
+                    nc.tensor.transpose(
+                        x_cols[:, block(a)], x_rows[s][:, a, block(j)], ident_bf16[:]
                     )
-                    nc.vector.scalar_tensor_tensor(
-                        out=xm_planes[:, j, :], in0=x_cols[:], scalar=curve[:, j : j + 1],
-                        in1=before[:], op0=ALU.mult, op1=ALU.add,
-                    )
+                nc.scalar.activation(
+                    out=shifted[j][:, 1:T], in_=x_cols[:, 0 : T - 1], func=ACT.Copy,
+                    scale=one_minus_curve[:, j : j + 1],
+                )
+                nc.vector.scalar_tensor_tensor(
+                    out=xm_planes[s][:, j, :], in0=x_cols[:], scalar=curve[:, j : j + 1],
+                    in1=shifted[j][:], op0=ALU.mult, op1=ALU.add,
+                )
+
+            def regroup_mix(s):
                 xm_grouped[s] = pairs.tile([P, T, PACK], BF16, name="xm_grouped", align_bytes=64)
                 nc.vector.tensor_copy(
                     out=xm_grouped[s][:].rearrange("p (c i) j -> p c j i", i=4),
-                    in_=xm_planes[:].rearrange("p j (c i) -> p c j i", i=4),
+                    in_=xm_planes[s][:].rearrange("p j (c i) -> p c j i", i=4),
                 )
 
             def quantise_mix(s):
@@ -167,17 +183,41 @@ def tile_rwkvtimemix_pa_t_kernel(
                     in_=xm_grouped[s][:].rearrange("p t j -> p (t j)"),
                 )
 
-            for s in range(SEQS):
-                mix(s)
-                if s > 0:
-                    quantise_mix(s - 1)
-            quantise_mix(SEQS - 1)
+            def gate_block(s, m):
+                r_bank = r_banks.tile([P, T], F32, name="r_bank")
+                product(r_bank, R_W, s, m)
+                nc.scalar.activation(out=gate[:, s, m, :], in_=r_bank[:], func=ACT.Sigmoid)
 
-        with tc.psum_pool(name="gate_banks", bufs=1, reuse_waits="tile") as gate_banks, tc.psum_pool(
-            name="state_banks", bufs=2, reuse_waits="tile"
-        ) as state_banks, tc.psum_pool(name="token_banks", bufs=3, reuse_waits="tile") as token_banks:
+            turn_weight(R_W)
+            quantise_weight(R_W)
+            for step in range(STEPS + GATE_LAG):
+                s, j = divmod(step, PACK)
+                if due(step, 0):
+                    mix_plane(s, j)
+                    if j == PACK - 1:
+                        regroup_mix(s)
+                        if s < len(LATER_WEIGHTS):
+                            turn_weight(LATER_WEIGHTS[s])
+                if due(step, 1) and j == 0:
+                    quantise_mix(s - 1)
+                    if s - 1 < len(LATER_WEIGHTS):
+                        quantise_weight(LATER_WEIGHTS[s - 1])
+                if due(step, GATE_LAG):
+                    gate_block(*divmod(step - GATE_LAG, PACK))
+
+        with ExitStack() as part:
+            triples = part.enter_context(tc.tile_pool(name="triples", bufs=3, reuse_waits="tile"))
+            quads = part.enter_context(tc.tile_pool(name="quads", bufs=4, reuse_waits="tile"))
+            k_banks = part.enter_context(tc.psum_pool(name="k_banks", bufs=1, reuse_waits="tile"))
+            v_banks = part.enter_context(tc.psum_pool(name="v_banks", bufs=2, reuse_waits="tile"))
+            state_banks = part.enter_context(
+                tc.psum_pool(name="state_banks", bufs=2, reuse_waits="tile")
+            )
+            token_banks = part.enter_context(
+                tc.psum_pool(name="token_banks", bufs=3, reuse_waits="tile")
+            )
+
             state_cols = {}
-            gate = {}
             new_state = {}
             h_grouped = {}
             h_codes = {}
@@ -191,31 +231,16 @@ def tile_rwkvtimemix_pa_t_kernel(
                         state_cols[step][:, block(a)], state_rows[s][:, a, block(m)], ident_bf16[:]
                     )
 
-            def product(bank, w, s, m):
-                nc.tensor.matmul_mx(
-                    out=bank[:],
-                    lhsT=w_codes[w][:, block(m)].bitcast(FP8X4),
-                    lhsT_scale=w_scales[w][:, block(m)],
-                    rhs=xm_codes[:, s, :].bitcast(FP8X4),
-                    rhs_scale=xm_scales[:, s, :],
-                    start=True,
-                    stop=True,
-                )
-
-            def gates(step):
+            def update_state(step):
                 s, m = divmod(step, PACK)
                 if m == 0:
-                    gate[s] = pairs.tile([P, PACK, T], F32, name="gate")
                     new_state[s] = triples.tile([P, PACK, T], F32, name="new_state")
-                v_bank = gate_banks.tile([P, T], F32, name="v_bank")
+                v_bank = v_banks.tile([P, T], F32, name="v_bank")
                 product(v_bank, V_W, s, m)
-                r_bank = gate_banks.tile([P, T], F32, name="r_bank")
-                product(r_bank, R_W, s, m)
-                k_bank = gate_banks.tile([P, T], F32, name="k_bank")
+                k_bank = k_banks.tile([P, T], F32, name="k_bank")
                 product(k_bank, K_W, s, m)
                 v_copy = triples.tile([P, T], F32, name="v_copy")
                 nc.scalar.copy(out=v_copy[:], in_=v_bank[:])
-                nc.scalar.activation(out=gate[s][:, m, :], in_=r_bank[:], func=ACT.Sigmoid)
                 kv = triples.tile([P, T], F32, name="kv")
                 nc.vector.tensor_tensor(out=kv[:], in0=k_bank[:], in1=v_copy[:], op=ALU.mult)
                 nc.vector.scalar_tensor_tensor(
@@ -228,14 +253,14 @@ def tile_rwkvtimemix_pa_t_kernel(
                 h_grouped[step] = triples.tile([P, P, PACK], BF16, name="h_grouped", align_bytes=64)
                 nc.vector.tensor_tensor(
                     out=h_grouped[step][:],
-                    in0=gate[s][:, :, block(a)].rearrange("p m t -> p t m"),
+                    in0=gate[:, s, :, block(a)].rearrange("p m t -> p t m"),
                     in1=new_state[s][:, :, block(a)].rearrange("p m t -> p t m"),
                     op=ALU.mult,
                 )
 
             def quantise_hidden(step):
-                h_codes[step] = triples.tile([P, P], U32, name="h_codes", align_bytes=64)
-                h_scales[step] = triples.tile([P, P], U8, name="h_scales", align_bytes=64)
+                h_codes[step] = quads.tile([P, P], U32, name="h_codes", align_bytes=64)
+                h_scales[step] = quads.tile([P, P], U8, name="h_scales", align_bytes=64)
                 nc.vector.quantize_mx(
                     out=h_codes[step][:].bitcast(FP8X4),
                     scales=h_scales[step][:],
@@ -249,7 +274,7 @@ def tile_rwkvtimemix_pa_t_kernel(
                     nc.tensor.transpose(
                         state_bank[:, block(m)], new_state[s][:, m, block(a)], ident_f32[:]
                     )
-                state_out = stores.tile([P, D], F32, name="state_out")
+                state_out = quads.tile([P, D], F32, name="state_out")
                 nc.scalar.copy(out=state_out[:], in_=state_bank[:])
                 nc.sync.dma_start(out=out_1[s, block(a), :], in_=state_out[:])
 
@@ -265,12 +290,9 @@ def tile_rwkvtimemix_pa_t_kernel(
                     start=True,
                     stop=True,
                 )
-                out_rows = stores.tile([P, D], F32, name="out_rows")
+                out_rows = quads.tile([P, D], F32, name="out_rows")
                 nc.scalar.copy(out=out_rows[:], in_=out_bank[:])
                 nc.sync.dma_start(out=out_0[s, block(a), :], in_=out_rows[:])
-
-            def due(step, lag):
-                return 0 <= step - lag < STEPS
 
             for step in range(STEPS + PROJECT_LAG):
                 if due(step, 0):
@@ -278,7 +300,7 @@ def tile_rwkvtimemix_pa_t_kernel(
                 if due(step, STATE_OUT_LAG):
                     return_state(step - STATE_OUT_LAG)
                 if due(step, 0):
-                    gates(step)
+                    update_state(step)
                 if due(step, QUANTISE_LAG):
                     quantise_hidden(step - QUANTISE_LAG)
                 if due(step, HIDDEN_LAG):

@@ -24,10 +24,12 @@ FLOPS = 2 * N_WEIGHTS * SEQS * T * D * D
 
 STEPS = SEQS * PACK
 GATE_LAG = PACK + 2
-HIDDEN_LAG = PACK
-QUANTISE_LAG = PACK + 1
-STATE_OUT_LAG = PACK + 1
-PROJECT_LAG = PACK + 3
+VALUE_LAG = PACK + 3
+UPDATE_LAG = PACK + 4
+HIDDEN_LAG = UPDATE_LAG + PACK
+QUANTISE_LAG = HIDDEN_LAG + 1
+STATE_OUT_LAG = UPDATE_LAG + PACK + 1
+PROJECT_LAG = QUANTISE_LAG + 2
 
 
 def block(i):
@@ -47,6 +49,13 @@ def tile_rwkvtimemix_pa_t_kernel(
     with ExitStack() as stack:
         stack.enter_context(tc.manual_schedule())
         keep = stack.enter_context(tc.tile_pool(name="keep", bufs=1))
+        pairs = stack.enter_context(tc.tile_pool(name="pairs", bufs=2))
+        triples = stack.enter_context(tc.tile_pool(name="triples", bufs=3))
+        quads = stack.enter_context(tc.tile_pool(name="quads", bufs=4))
+        scalar_banks = stack.enter_context(tc.psum_pool(name="scalar_banks", bufs=3))
+        product_banks = stack.enter_context(tc.psum_pool(name="product_banks", bufs=2))
+        turned_banks = stack.enter_context(tc.psum_pool(name="turned_banks", bufs=2))
+        key_bank = stack.enter_context(tc.psum_pool(name="key_bank", bufs=1))
 
         def load_rows(rows, matrix):
             nc.sync.dma_start(out=rows[:], in_=matrix.rearrange("(a p) c -> p a c", p=P))
@@ -57,6 +66,18 @@ def tile_rwkvtimemix_pa_t_kernel(
         nc.sync.dma_start(
             out=vec_rows[PACK : 2 * PACK, :], in_=time_curve.rearrange("(j p) -> j p", p=P)
         )
+        w_rows = [keep.tile([P, PACK, D], BF16, name="w_rows%d" % w) for w in range(N_WEIGHTS)]
+        x_rows = [keep.tile([P, PACK, D], BF16, name="x_rows%d" % s) for s in range(SEQS)]
+        state_rows = [keep.tile([P, PACK, D], BF16, name="state_rows%d" % s) for s in range(SEQS)]
+        load_rows(w_rows[R_W], weights[R_W])
+        for s in range(SEQS):
+            load_rows(x_rows[s], x[s])
+            if s < len(LATER_WEIGHTS):
+                load_rows(w_rows[LATER_WEIGHTS[s]], weights[LATER_WEIGHTS[s]])
+            else:
+                load_rows(state_rows[s - len(LATER_WEIGHTS)], state[s - len(LATER_WEIGHTS)])
+        for s in range(SEQS - len(LATER_WEIGHTS), SEQS):
+            load_rows(state_rows[s], state[s])
 
         ident_bf16 = keep.tile([P, P], BF16, name="ident_bf16")
         make_identity(nc, ident_bf16[:])
@@ -72,9 +93,89 @@ def tile_rwkvtimemix_pa_t_kernel(
         xm_codes = keep.tile([P, SEQS, T], U32, name="xm_codes", align_bytes=64)
         xm_scales = keep.tile([P, SEQS, T], U8, name="xm_scales", align_bytes=64)
 
-        state_rows = [keep.tile([P, PACK, D], BF16, name="state_rows%d" % s) for s in range(SEQS)]
-        gate = keep.tile([P, SEQS, PACK, T], F32, name="gate")
+        shifted = [keep.tile([P, T], F32, name="shifted%d" % j) for j in range(PACK)]
+        for j in range(PACK):
+            nc.vector.memset(shifted[j][:], 0.0)
+
+        vec_cols = key_bank.tile([P, P], BF16, name="vec_cols", tag="key")
+        nc.tensor.transpose(vec_cols[:], vec_rows[:], ident_bf16[:])
+        per_channel = keep.tile([P, 2 * PACK], F32, name="per_channel")
+        nc.vector.tensor_copy(out=per_channel[:], in_=vec_cols[:, 0 : 2 * PACK])
+        curve = per_channel[:, PACK : 2 * PACK]
+        one_minus_curve = keep.tile([P, PACK], F32, name="one_minus_curve")
+        nc.vector.tensor_scalar(
+            out=one_minus_curve[:], in0=curve, scalar1=-1.0, scalar2=1.0,
+            op0=ALU.mult, op1=ALU.add,
+        )
+        rate = keep.tile([P, PACK], F32, name="rate")
+        nc.scalar.activation(out=rate[:], in_=per_channel[:, 0:PACK], func=ACT.Exp)
         decay = keep.tile([P, PACK], F32, name="decay")
+        nc.scalar.activation(out=decay[:], in_=rate[:], func=ACT.Exp, scale=-1.0)
+
+        w_grouped = {}
+        xm_planes = {}
+        xm_grouped = {}
+        gate = {}
+        v_copy = {}
+        kv = {}
+        state_cols = {}
+        new_state = {}
+        h_grouped = {}
+        h_codes = {}
+        h_scales = {}
+
+        def turn_weight(w):
+            w_grouped[w] = pairs.tile([P, D, PACK], BF16, name="w_grouped", align_bytes=64)
+            for half in range(2):
+                w_cols = turned_banks.tile([P, 2, PACK, P], BF16, name="w_cols", tag="turned")
+                for b in range(2):
+                    for j in range(PACK):
+                        nc.tensor.transpose(
+                            w_cols[:, b, j, :], w_rows[w][:, 2 * half + b, block(j)], ident_bf16[:]
+                        )
+                copy = nc.vector.tensor_copy if half == 0 else nc.scalar.copy
+                copy(
+                    out=w_grouped[w][:, 2 * half * P : 2 * (half + 1) * P, :].rearrange(
+                        "p (b o) j -> p b o j", b=2
+                    ),
+                    in_=w_cols[:].rearrange("p b j o -> p b o j"),
+                )
+
+        def quantise_weight(w):
+            nc.vector.quantize_mx(
+                out=w_codes[w][:].bitcast(FP8X4),
+                scales=w_scales[w][:],
+                in_=w_grouped[w][:].rearrange("p o j -> p (o j)"),
+            )
+
+        def mix_plane(s, j):
+            if j == 0:
+                xm_planes[s] = pairs.tile([P, PACK, T], BF16, name="xm_planes")
+            x_cols = scalar_banks.tile([P, T], BF16, name="x_cols", tag="scalar")
+            for a in range(PACK):
+                nc.tensor.transpose(x_cols[:, block(a)], x_rows[s][:, a, block(j)], ident_bf16[:])
+            nc.scalar.activation(
+                out=shifted[j][:, 1:T], in_=x_cols[:, 0 : T - 1], func=ACT.Copy,
+                scale=one_minus_curve[:, j : j + 1],
+            )
+            nc.vector.scalar_tensor_tensor(
+                out=xm_planes[s][:, j, :], in0=x_cols[:], scalar=curve[:, j : j + 1],
+                in1=shifted[j][:], op0=ALU.mult, op1=ALU.add,
+            )
+
+        def regroup_mix(s):
+            xm_grouped[s] = pairs.tile([P, T, PACK], BF16, name="xm_grouped", align_bytes=64)
+            nc.vector.tensor_copy(
+                out=xm_grouped[s][:].rearrange("p (c i) j -> p c j i", i=4),
+                in_=xm_planes[s][:].rearrange("p j (c i) -> p c j i", i=4),
+            )
+
+        def quantise_mix(s):
+            nc.vector.quantize_mx(
+                out=xm_codes[:, s, :].bitcast(FP8X4),
+                scales=xm_scales[:, s, :],
+                in_=xm_grouped[s][:].rearrange("p t j -> p (t j)"),
+            )
 
         def product(bank, w, s, m):
             nc.tensor.matmul_mx(
@@ -87,223 +188,114 @@ def tile_rwkvtimemix_pa_t_kernel(
                 stop=True,
             )
 
-        with ExitStack() as part:
-            rows = part.enter_context(tc.tile_pool(name="rows", bufs=1))
-            pairs = part.enter_context(tc.tile_pool(name="pairs", bufs=2))
-            vec_bank = part.enter_context(tc.psum_pool(name="vec_bank", bufs=1))
-            w_banks = part.enter_context(tc.psum_pool(name="w_banks", bufs=2))
-            x_banks = part.enter_context(tc.psum_pool(name="x_banks", bufs=3))
-            r_banks = part.enter_context(tc.psum_pool(name="r_banks", bufs=2))
+        def gate_block(s, m):
+            if m == 0:
+                gate[s] = triples.tile([P, PACK, T], F32, name="gate")
+            r_bank = product_banks.tile([P, T], F32, name="r_bank", tag="product")
+            product(r_bank, R_W, s, m)
+            nc.scalar.activation(out=gate[s][:, m, :], in_=r_bank[:], func=ACT.Sigmoid)
 
-            w_rows = [rows.tile([P, PACK, D], BF16, name="w_rows%d" % w) for w in range(N_WEIGHTS)]
-            x_rows = [rows.tile([P, PACK, D], BF16, name="x_rows%d" % s) for s in range(SEQS)]
-            load_rows(w_rows[R_W], weights[R_W])
-            for s in range(SEQS):
-                load_rows(x_rows[s], x[s])
-                if s < len(LATER_WEIGHTS):
-                    load_rows(w_rows[LATER_WEIGHTS[s]], weights[LATER_WEIGHTS[s]])
-            for s in range(SEQS):
-                load_rows(state_rows[s], state[s])
+        def value_block(s, m):
+            v_bank = product_banks.tile([P, T], F32, name="v_bank", tag="product")
+            product(v_bank, V_W, s, m)
+            v_copy[s, m] = quads.tile([P, T], F32, name="v_copy")
+            nc.scalar.copy(out=v_copy[s, m][:], in_=v_bank[:])
 
-            shifted = [rows.tile([P, T], F32, name="shifted%d" % j) for j in range(PACK)]
-            for j in range(PACK):
-                nc.vector.memset(shifted[j][:], 0.0)
+        def turn_state(s, m):
+            state_cols[s, m] = turned_banks.tile([P, T], BF16, name="state_cols", tag="turned")
+            for a in range(PACK):
+                nc.tensor.transpose(
+                    state_cols[s, m][:, block(a)], state_rows[s][:, a, block(m)], ident_bf16[:]
+                )
 
-            vec_cols = vec_bank.tile([P, P], BF16, name="vec_cols")
-            nc.tensor.transpose(vec_cols[:], vec_rows[:], ident_bf16[:])
-            per_channel = rows.tile([P, 2 * PACK], F32, name="per_channel")
-            nc.vector.tensor_copy(out=per_channel[:], in_=vec_cols[:, 0 : 2 * PACK])
-            curve = per_channel[:, PACK : 2 * PACK]
-            one_minus_curve = rows.tile([P, PACK], F32, name="one_minus_curve")
-            nc.vector.tensor_scalar(
-                out=one_minus_curve[:], in0=curve, scalar1=-1.0, scalar2=1.0,
-                op0=ALU.mult, op1=ALU.add,
+        def key_times_value(s, m):
+            k_bank = key_bank.tile([P, T], F32, name="k_bank", tag="key")
+            product(k_bank, K_W, s, m)
+            kv[s, m] = triples.tile([P, T], F32, name="kv")
+            nc.vector.tensor_tensor(out=kv[s, m][:], in0=k_bank[:], in1=v_copy[s, m][:], op=ALU.mult)
+
+        def update_state(s, m):
+            if m == 0:
+                new_state[s] = triples.tile([P, PACK, T], F32, name="new_state")
+            nc.vector.scalar_tensor_tensor(
+                out=new_state[s][:, m, :], in0=state_cols[s, m][:], scalar=decay[:, m : m + 1],
+                in1=kv[s, m][:], op0=ALU.mult, op1=ALU.add,
             )
-            rate = rows.tile([P, PACK], F32, name="rate")
-            nc.scalar.activation(out=rate[:], in_=per_channel[:, 0:PACK], func=ACT.Exp)
-            nc.scalar.activation(out=decay[:], in_=rate[:], func=ACT.Exp, scale=-1.0)
 
-            w_grouped = {}
+        def hidden(s, a):
+            h_grouped[s, a] = triples.tile([P, P, PACK], BF16, name="h_grouped", align_bytes=64)
+            nc.vector.tensor_tensor(
+                out=h_grouped[s, a][:],
+                in0=gate[s][:, :, block(a)].rearrange("p m t -> p t m"),
+                in1=new_state[s][:, :, block(a)].rearrange("p m t -> p t m"),
+                op=ALU.mult,
+            )
 
-            def turn_weight(w):
-                w_grouped[w] = pairs.tile([P, D, PACK], BF16, name="w_grouped", align_bytes=64)
-                for half in range(2):
-                    w_cols = w_banks.tile([P, 2, PACK, P], BF16, name="w_cols")
-                    for b in range(2):
-                        for j in range(PACK):
-                            nc.tensor.transpose(
-                                w_cols[:, b, j, :], w_rows[w][:, 2 * half + b, block(j)],
-                                ident_bf16[:],
-                            )
-                    nc.vector.tensor_copy(
-                        out=w_grouped[w][:, 2 * half * P : 2 * (half + 1) * P, :].rearrange(
-                            "p (b o) j -> p b o j", b=2
-                        ),
-                        in_=w_cols[:].rearrange("p b j o -> p b o j"),
-                    )
+        def quantise_hidden(s, a):
+            h_codes[s, a] = quads.tile([P, P], U32, name="h_codes", align_bytes=64)
+            h_scales[s, a] = quads.tile([P, P], U8, name="h_scales", align_bytes=64)
+            nc.vector.quantize_mx(
+                out=h_codes[s, a][:].bitcast(FP8X4),
+                scales=h_scales[s, a][:],
+                in_=h_grouped[s, a][:].rearrange("p t m -> p (t m)"),
+            )
 
-            def quantise_weight(w):
-                nc.vector.quantize_mx(
-                    out=w_codes[w][:].bitcast(FP8X4),
-                    scales=w_scales[w][:],
-                    in_=w_grouped[w][:].rearrange("p o j -> p (o j)"),
+        def return_state(s, a):
+            state_bank = scalar_banks.tile([P, D], F32, name="state_bank", tag="scalar")
+            for m in range(PACK):
+                nc.tensor.transpose(
+                    state_bank[:, block(m)], new_state[s][:, m, block(a)], ident_f32[:]
                 )
+            state_out = quads.tile([P, D], F32, name="state_out")
+            nc.scalar.copy(out=state_out[:], in_=state_bank[:])
+            nc.sync.dma_start(out=out_1[s, block(a), :], in_=state_out[:])
 
-            xm_planes = {}
-            xm_grouped = {}
+        def project(s, a):
+            out_bank = scalar_banks.tile([P, D], F32, name="out_bank", tag="scalar")
+            nc.tensor.matmul_mx(
+                out=out_bank[:],
+                lhsT=h_codes[s, a][:].bitcast(FP8X4),
+                lhsT_scale=h_scales[s, a][:],
+                rhs=w_codes[O_W][:].bitcast(FP8X4),
+                rhs_scale=w_scales[O_W][:],
+                start=True,
+                stop=True,
+            )
+            out_rows = quads.tile([P, D], F32, name="out_rows")
+            nc.scalar.copy(out=out_rows[:], in_=out_bank[:])
+            nc.sync.dma_start(out=out_0[s, block(a), :], in_=out_rows[:])
 
-            def mix_plane(s, j):
-                if j == 0:
-                    xm_planes[s] = pairs.tile([P, PACK, T], BF16, name="xm_planes")
-                x_cols = x_banks.tile([P, T], BF16, name="x_cols")
-                for a in range(PACK):
-                    nc.tensor.transpose(
-                        x_cols[:, block(a)], x_rows[s][:, a, block(j)], ident_bf16[:]
-                    )
-                nc.scalar.activation(
-                    out=shifted[j][:, 1:T], in_=x_cols[:, 0 : T - 1], func=ACT.Copy,
-                    scale=one_minus_curve[:, j : j + 1],
-                )
-                nc.vector.scalar_tensor_tensor(
-                    out=xm_planes[s][:, j, :], in0=x_cols[:], scalar=curve[:, j : j + 1],
-                    in1=shifted[j][:], op0=ALU.mult, op1=ALU.add,
-                )
-
-            def regroup_mix(s):
-                xm_grouped[s] = pairs.tile([P, T, PACK], BF16, name="xm_grouped", align_bytes=64)
-                nc.vector.tensor_copy(
-                    out=xm_grouped[s][:].rearrange("p (c i) j -> p c j i", i=4),
-                    in_=xm_planes[s][:].rearrange("p j (c i) -> p c j i", i=4),
-                )
-
-            def quantise_mix(s):
-                nc.vector.quantize_mx(
-                    out=xm_codes[:, s, :].bitcast(FP8X4),
-                    scales=xm_scales[:, s, :],
-                    in_=xm_grouped[s][:].rearrange("p t j -> p (t j)"),
-                )
-
-            def gate_block(s, m):
-                r_bank = r_banks.tile([P, T], F32, name="r_bank")
-                product(r_bank, R_W, s, m)
-                nc.scalar.activation(out=gate[:, s, m, :], in_=r_bank[:], func=ACT.Sigmoid)
-
-            turn_weight(R_W)
-            quantise_weight(R_W)
-            for step in range(STEPS + GATE_LAG):
+        turn_weight(R_W)
+        quantise_weight(R_W)
+        for step in range(STEPS + PROJECT_LAG):
+            if due(step, 0):
                 s, j = divmod(step, PACK)
-                if due(step, 0):
-                    mix_plane(s, j)
-                    if j == PACK - 1:
-                        regroup_mix(s)
-                        if s < len(LATER_WEIGHTS):
-                            turn_weight(LATER_WEIGHTS[s])
-                if due(step, 1) and j == 0:
-                    quantise_mix(s - 1)
-                    if s - 1 < len(LATER_WEIGHTS):
-                        quantise_weight(LATER_WEIGHTS[s - 1])
-                if due(step, GATE_LAG):
-                    gate_block(*divmod(step - GATE_LAG, PACK))
-
-        with ExitStack() as part:
-            triples = part.enter_context(tc.tile_pool(name="triples", bufs=3, reuse_waits="tile"))
-            quads = part.enter_context(tc.tile_pool(name="quads", bufs=4, reuse_waits="tile"))
-            k_banks = part.enter_context(tc.psum_pool(name="k_banks", bufs=1, reuse_waits="tile"))
-            v_banks = part.enter_context(tc.psum_pool(name="v_banks", bufs=2, reuse_waits="tile"))
-            state_banks = part.enter_context(
-                tc.psum_pool(name="state_banks", bufs=2, reuse_waits="tile")
-            )
-            token_banks = part.enter_context(
-                tc.psum_pool(name="token_banks", bufs=3, reuse_waits="tile")
-            )
-
-            state_cols = {}
-            new_state = {}
-            h_grouped = {}
-            h_codes = {}
-            h_scales = {}
-
-            def turn_state(step):
-                s, m = divmod(step, PACK)
-                state_cols[step] = state_banks.tile([P, T], BF16, name="state_cols")
-                for a in range(PACK):
-                    nc.tensor.transpose(
-                        state_cols[step][:, block(a)], state_rows[s][:, a, block(m)], ident_bf16[:]
-                    )
-
-            def update_state(step):
-                s, m = divmod(step, PACK)
-                if m == 0:
-                    new_state[s] = triples.tile([P, PACK, T], F32, name="new_state")
-                v_bank = v_banks.tile([P, T], F32, name="v_bank")
-                product(v_bank, V_W, s, m)
-                k_bank = k_banks.tile([P, T], F32, name="k_bank")
-                product(k_bank, K_W, s, m)
-                v_copy = triples.tile([P, T], F32, name="v_copy")
-                nc.scalar.copy(out=v_copy[:], in_=v_bank[:])
-                kv = triples.tile([P, T], F32, name="kv")
-                nc.vector.tensor_tensor(out=kv[:], in0=k_bank[:], in1=v_copy[:], op=ALU.mult)
-                nc.vector.scalar_tensor_tensor(
-                    out=new_state[s][:, m, :], in0=state_cols[step][:],
-                    scalar=decay[:, m : m + 1], in1=kv[:], op0=ALU.mult, op1=ALU.add,
-                )
-
-            def hidden(step):
-                s, a = divmod(step, PACK)
-                h_grouped[step] = triples.tile([P, P, PACK], BF16, name="h_grouped", align_bytes=64)
-                nc.vector.tensor_tensor(
-                    out=h_grouped[step][:],
-                    in0=gate[:, s, :, block(a)].rearrange("p m t -> p t m"),
-                    in1=new_state[s][:, :, block(a)].rearrange("p m t -> p t m"),
-                    op=ALU.mult,
-                )
-
-            def quantise_hidden(step):
-                h_codes[step] = quads.tile([P, P], U32, name="h_codes", align_bytes=64)
-                h_scales[step] = quads.tile([P, P], U8, name="h_scales", align_bytes=64)
-                nc.vector.quantize_mx(
-                    out=h_codes[step][:].bitcast(FP8X4),
-                    scales=h_scales[step][:],
-                    in_=h_grouped[step][:].rearrange("p t m -> p (t m)"),
-                )
-
-            def return_state(step):
-                s, a = divmod(step, PACK)
-                state_bank = token_banks.tile([P, D], F32, name="token_bank")
-                for m in range(PACK):
-                    nc.tensor.transpose(
-                        state_bank[:, block(m)], new_state[s][:, m, block(a)], ident_f32[:]
-                    )
-                state_out = quads.tile([P, D], F32, name="state_out")
-                nc.scalar.copy(out=state_out[:], in_=state_bank[:])
-                nc.sync.dma_start(out=out_1[s, block(a), :], in_=state_out[:])
-
-            def project(step):
-                s, a = divmod(step, PACK)
-                out_bank = token_banks.tile([P, D], F32, name="token_bank")
-                nc.tensor.matmul_mx(
-                    out=out_bank[:],
-                    lhsT=h_codes[step][:].bitcast(FP8X4),
-                    lhsT_scale=h_scales[step][:],
-                    rhs=w_codes[O_W][:].bitcast(FP8X4),
-                    rhs_scale=w_scales[O_W][:],
-                    start=True,
-                    stop=True,
-                )
-                out_rows = quads.tile([P, D], F32, name="out_rows")
-                nc.scalar.copy(out=out_rows[:], in_=out_bank[:])
-                nc.sync.dma_start(out=out_0[s, block(a), :], in_=out_rows[:])
-
-            for step in range(STEPS + PROJECT_LAG):
-                if due(step, 0):
-                    turn_state(step)
-                if due(step, STATE_OUT_LAG):
-                    return_state(step - STATE_OUT_LAG)
-                if due(step, 0):
-                    update_state(step)
-                if due(step, QUANTISE_LAG):
-                    quantise_hidden(step - QUANTISE_LAG)
-                if due(step, HIDDEN_LAG):
-                    hidden(step - HIDDEN_LAG)
-                if due(step, PROJECT_LAG):
-                    project(step - PROJECT_LAG)
+                mix_plane(s, j)
+                if j == PACK - 1:
+                    regroup_mix(s)
+                if step % 2 == 1 and step // 2 < len(LATER_WEIGHTS):
+                    turn_weight(LATER_WEIGHTS[step // 2])
+            if due(step, 1):
+                s, j = divmod(step - 1, PACK)
+                if j == PACK - 1:
+                    quantise_mix(s)
+                if (step - 1) % 2 == 1 and (step - 1) // 2 < len(LATER_WEIGHTS):
+                    quantise_weight(LATER_WEIGHTS[(step - 1) // 2])
+            if due(step, UPDATE_LAG):
+                turn_state(*divmod(step - UPDATE_LAG, PACK))
+            if due(step, STATE_OUT_LAG):
+                return_state(*divmod(step - STATE_OUT_LAG, PACK))
+            if due(step, GATE_LAG):
+                gate_block(*divmod(step - GATE_LAG, PACK))
+            if due(step, VALUE_LAG):
+                value_block(*divmod(step - VALUE_LAG, PACK))
+            if due(step, UPDATE_LAG):
+                key_times_value(*divmod(step - UPDATE_LAG, PACK))
+            if due(step, HIDDEN_LAG):
+                hidden(*divmod(step - HIDDEN_LAG, PACK))
+            if due(step, UPDATE_LAG):
+                update_state(*divmod(step - UPDATE_LAG, PACK))
+            if due(step, QUANTISE_LAG):
+                quantise_hidden(*divmod(step - QUANTISE_LAG, PACK))
+            if due(step, PROJECT_LAG):
+                project(*divmod(step - PROJECT_LAG, PACK))

@@ -225,9 +225,9 @@ def tile_rwkvtimemix_pa_t_kernel(
         def hidden(s, a):
             h_grouped[s, a] = triples.tile([P, P, PACK], BF16, name="h_grouped", align_bytes=64)
             nc.vector.tensor_tensor(
-                out=h_grouped[s, a][:],
-                in0=gate[s][:, :, block(a)].rearrange("p m t -> p t m"),
-                in1=new_state[s][:, :, block(a)].rearrange("p m t -> p t m"),
+                out=h_grouped[s, a][:].rearrange("p (c i) m -> p c m i", i=4),
+                in0=gate[s][:, :, block(a)].rearrange("p m (c i) -> p c m i", i=4),
+                in1=new_state[s][:, :, block(a)].rearrange("p m (c i) -> p c m i", i=4),
                 op=ALU.mult,
             )
 

@@ -47,7 +47,6 @@ def tile_rwkvtimemix_pa_t_kernel(
     weights = (Wk, Wv, Wr, Wo)
 
     with ExitStack() as stack:
-        stack.enter_context(tc.manual_schedule())
         keep = stack.enter_context(tc.tile_pool(name="keep", bufs=1))
         pairs = stack.enter_context(tc.tile_pool(name="pairs", bufs=2))
         triples = stack.enter_context(tc.tile_pool(name="triples", bufs=3))

@@ -23,6 +23,7 @@ LATER_WEIGHTS = (V_W, K_W, O_W)
 FLOPS = 2 * N_WEIGHTS * SEQS * T * D * D
 
 STEPS = SEQS * PACK
+TILES = 2
 GATE_LAG = PACK + 2
 VALUE_LAG = PACK + 3
 UPDATE_LAG = PACK + 4
@@ -222,17 +223,18 @@ def tile_rwkvtimemix_pa_t_kernel(
             )
 
         def hidden(s, a):
-            h_grouped[s, a] = triples.tile([P, P, PACK], BF16, name="h_grouped", align_bytes=64)
+            h_grouped[s, a] = triples.tile([P, TILES * P, PACK], BF16, name="h_grouped", align_bytes=64)
+            tokens = slice(a * P, (a + TILES) * P)
             nc.vector.tensor_tensor(
                 out=h_grouped[s, a][:].rearrange("p (c i) m -> p c m i", i=4),
-                in0=gate[s][:, :, block(a)].rearrange("p m (c i) -> p c m i", i=4),
-                in1=new_state[s][:, :, block(a)].rearrange("p m (c i) -> p c m i", i=4),
+                in0=gate[s][:, :, tokens].rearrange("p m (c i) -> p c m i", i=4),
+                in1=new_state[s][:, :, tokens].rearrange("p m (c i) -> p c m i", i=4),
                 op=ALU.mult,
             )
 
         def quantise_hidden(s, a):
-            h_codes[s, a] = quads.tile([P, P], U32, name="h_codes", align_bytes=64)
-            h_scales[s, a] = quads.tile([P, P], U8, name="h_scales", align_bytes=64)
+            h_codes[s, a] = triples.tile([P, TILES * P], U32, name="h_codes", align_bytes=64)
+            h_scales[s, a] = triples.tile([P, TILES * P], U8, name="h_scales", align_bytes=64)
             nc.vector.quantize_mx(
                 out=h_codes[s, a][:].bitcast(FP8X4),
                 scales=h_scales[s, a][:],
@@ -253,8 +255,8 @@ def tile_rwkvtimemix_pa_t_kernel(
             out_bank = scalar_banks.tile([P, D], F32, name="out_bank", tag="scalar")
             nc.tensor.matmul_mx(
                 out=out_bank[:],
-                lhsT=h_codes[s, a][:].bitcast(FP8X4),
-                lhsT_scale=h_scales[s, a][:],
+                lhsT=h_codes[s, a - a % TILES][:, block(a % TILES)].bitcast(FP8X4),
+                lhsT_scale=h_scales[s, a - a % TILES][:, block(a % TILES)],
                 rhs=w_codes[O_W][:].bitcast(FP8X4),
                 rhs_scale=w_scales[O_W][:],
                 start=True,
@@ -290,11 +292,11 @@ def tile_rwkvtimemix_pa_t_kernel(
                 value_block(*divmod(step - VALUE_LAG, PACK))
             if due(step, UPDATE_LAG):
                 key_times_value(*divmod(step - UPDATE_LAG, PACK))
-            if due(step, HIDDEN_LAG):
+            if due(step, HIDDEN_LAG) and (step - HIDDEN_LAG) % TILES == 0:
                 hidden(*divmod(step - HIDDEN_LAG, PACK))
             if due(step, UPDATE_LAG):
                 update_state(*divmod(step - UPDATE_LAG, PACK))
-            if due(step, QUANTISE_LAG):
+            if due(step, QUANTISE_LAG) and (step - QUANTISE_LAG) % TILES == 0:
                 quantise_hidden(*divmod(step - QUANTISE_LAG, PACK))
             if due(step, PROJECT_LAG):
                 project(*divmod(step - PROJECT_LAG, PACK))

@@ -69,9 +69,10 @@ def tile_rwkvtimemix_pa_t_kernel(
         w_rows = [keep.tile([P, PACK, D], BF16, name="w_rows%d" % w) for w in range(N_WEIGHTS)]
         x_rows = [keep.tile([P, PACK, D], BF16, name="x_rows%d" % s) for s in range(SEQS)]
         state_rows = [keep.tile([P, PACK, D], BF16, name="state_rows%d" % s) for s in range(SEQS)]
-        load_rows(w_rows[R_W], weights[R_W])
         for s in range(SEQS):
             load_rows(x_rows[s], x[s])
+            if s == 0:
+                load_rows(w_rows[R_W], weights[R_W])
             if s < len(LATER_WEIGHTS):
                 load_rows(w_rows[LATER_WEIGHTS[s]], weights[LATER_WEIGHTS[s]])
             else:
@@ -95,7 +96,7 @@ def tile_rwkvtimemix_pa_t_kernel(
 
         shifted = [keep.tile([P, T], F32, name="shifted%d" % j) for j in range(PACK)]
         for j in range(PACK):
-            nc.vector.memset(shifted[j][:], 0.0)
+            nc.vector.memset(shifted[j][:, 0:1], 0.0)
 
         vec_cols = key_bank.tile([P, P], BF16, name="vec_cols", tag="key")
         nc.tensor.transpose(vec_cols[:], vec_rows[:], ident_bf16[:])
@@ -151,9 +152,12 @@ def tile_rwkvtimemix_pa_t_kernel(
         def mix_plane(s, j):
             if j == 0:
                 xm_planes[s] = pairs.tile([P, PACK, T], BF16, name="xm_planes")
-            x_cols = scalar_banks.tile([P, T], BF16, name="x_cols", tag="scalar")
+            x_cols = scalar_banks.tile([P, T], F32, name="x_cols", tag="scalar")
             for a in range(PACK):
-                nc.tensor.transpose(x_cols[:, block(a)], x_rows[s][:, a, block(j)], ident_bf16[:])
+                nc.tensor.matmul(
+                    x_cols[:, block(a)], lhsT=x_rows[s][:, a, block(j)], rhs=ident_bf16[:],
+                    start=True, stop=True,
+                )
             nc.scalar.activation(
                 out=shifted[j][:, 1:T], in_=x_cols[:, 0 : T - 1], func=ACT.Copy,
                 scale=one_minus_curve[:, j : j + 1],
@@ -266,8 +270,6 @@ def tile_rwkvtimemix_pa_t_kernel(
             nc.scalar.copy(out=out_rows[:], in_=out_bank[:])
             nc.sync.dma_start(out=out_0[s, block(a), :], in_=out_rows[:])
 
-        turn_weight(R_W)
-        quantise_weight(R_W)
         for step in range(STEPS + PROJECT_LAG):
             if due(step, 0):
                 s, j = divmod(step, PACK)
@@ -276,7 +278,11 @@ def tile_rwkvtimemix_pa_t_kernel(
                     regroup_mix(s)
                 if step % 2 == 1 and step // 2 < len(LATER_WEIGHTS):
                     turn_weight(LATER_WEIGHTS[step // 2])
+                if step == 0:
+                    turn_weight(R_W)
             if due(step, 1):
+                if step == 1:
+                    quantise_weight(R_W)
                 s, j = divmod(step - 1, PACK)
                 if j == PACK - 1:
                     quantise_mix(s)

@@ -23,6 +23,7 @@ LATER_WEIGHTS = (V_W, K_W, O_W)
 FLOPS = 2 * N_WEIGHTS * SEQS * T * D * D
 
 STEPS = SEQS * PACK
+RUN = 4
 TILES = 2
 GATE_LAG = PACK + 2
 VALUE_LAG = PACK + 3
@@ -35,6 +36,10 @@ PROJECT_LAG = QUANTISE_LAG + 2
 
 def block(i):
     return slice(i * P, (i + 1) * P)
+
+
+def runs(a, tiles):
+    return slice(a * P // RUN, (a + tiles) * P // RUN)
 
 
 def due(step, lag):
@@ -169,10 +174,12 @@ def tile_rwkvtimemix_pa_t_kernel(
 
         def regroup_mix(s):
             xm_grouped[s] = pairs.tile([P, T, PACK], BF16, name="xm_grouped", align_bytes=64)
-            nc.vector.tensor_copy(
-                out=xm_grouped[s][:].rearrange("p (c i) j -> p c j i", i=4),
-                in_=xm_planes[s][:].rearrange("p j (c i) -> p c j i", i=4),
-            )
+            for a in range(PACK):
+                nc.gpsimd.tensor_scalar(
+                    out=xm_grouped[s][:, block(a), :],
+                    in0=xm_planes[s][:, :, block(a)].rearrange("p j t -> p t j"),
+                    scalar1=1.0, scalar2=0.0, op0=ALU.mult, op1=ALU.add,
+                )
 
         def quantise_mix(s):
             nc.vector.quantize_mx(
@@ -181,27 +188,32 @@ def tile_rwkvtimemix_pa_t_kernel(
                 in_=xm_grouped[s][:].rearrange("p t j -> p (t j)"),
             )
 
-        def product(bank, w, s, m):
+        def product(bank, w, s, m, tokens):
             nc.tensor.matmul_mx(
-                out=bank[:],
+                out=bank,
                 lhsT=w_codes[w][:, block(m)].bitcast(FP8X4),
                 lhsT_scale=w_scales[w][:, block(m)],
-                rhs=xm_codes[:, s, :].bitcast(FP8X4),
-                rhs_scale=xm_scales[:, s, :],
+                rhs=xm_codes[:, s, tokens].bitcast(FP8X4),
+                rhs_scale=xm_scales[:, s, tokens],
                 start=True,
                 stop=True,
             )
 
-        def gate_block(s, m):
-            if m == 0:
-                gate[s] = triples.tile([P, PACK, T], F32, name="gate")
-            r_bank = product_banks.tile([P, T], F32, name="r_bank", tag="product")
-            product(r_bank, R_W, s, m)
-            nc.scalar.activation(out=gate[s][:, m, :], in_=r_bank[:], func=ACT.Sigmoid)
+        def gate_tile(s, a):
+            if a == 0:
+                gate[s] = triples.tile([P, T // RUN, PACK, RUN], F32, name="gate")
+            r_bank = product_banks.tile([P, PACK, P], F32, name="r_bank", tag="product")
+            for m in range(PACK):
+                product(r_bank[:, m, :], R_W, s, m, block(a))
+            nc.scalar.activation(
+                out=gate[s][:, runs(a, 1), :, :],
+                in_=r_bank[:].rearrange("p m (c i) -> p c m i", i=RUN),
+                func=ACT.Sigmoid,
+            )
 
         def value_block(s, m):
             v_bank = product_banks.tile([P, T], F32, name="v_bank", tag="product")
-            product(v_bank, V_W, s, m)
+            product(v_bank[:], V_W, s, m, slice(0, T))
             v_copy[s, m] = quads.tile([P, T], F32, name="v_copy")
             nc.scalar.copy(out=v_copy[s, m][:], in_=v_bank[:])
 
@@ -214,7 +226,7 @@ def tile_rwkvtimemix_pa_t_kernel(
 
         def key_times_value(s, m):
             k_bank = key_bank.tile([P, T], F32, name="k_bank", tag="key")
-            product(k_bank, K_W, s, m)
+            product(k_bank[:], K_W, s, m, slice(0, T))
             kv[s, m] = triples.tile([P, T], F32, name="kv")
             nc.vector.tensor_tensor(out=kv[s, m][:], in0=k_bank[:], in1=v_copy[s, m][:], op=ALU.mult)
 
@@ -230,9 +242,9 @@ def tile_rwkvtimemix_pa_t_kernel(
             h_grouped[s, a] = triples.tile([P, TILES * P, PACK], BF16, name="h_grouped", align_bytes=64)
             tokens = slice(a * P, (a + TILES) * P)
             nc.vector.tensor_tensor(
-                out=h_grouped[s, a][:].rearrange("p (c i) m -> p c m i", i=4),
-                in0=gate[s][:, :, tokens].rearrange("p m (c i) -> p c m i", i=4),
-                in1=new_state[s][:, :, tokens].rearrange("p m (c i) -> p c m i", i=4),
+                out=h_grouped[s, a][:].rearrange("p (c i) m -> p c m i", i=RUN),
+                in0=gate[s][:, runs(a, TILES), :, :],
+                in1=new_state[s][:, :, tokens].rearrange("p m (c i) -> p c m i", i=RUN),
                 op=ALU.mult,
             )
 
@@ -280,12 +292,11 @@ def tile_rwkvtimemix_pa_t_kernel(
                     turn_weight(LATER_WEIGHTS[step // 2])
                 if step == 0:
                     turn_weight(R_W)
+            if due(step, 2) and (step - 2) % PACK == PACK - 1:
+                quantise_mix((step - 2) // PACK)
             if due(step, 1):
                 if step == 1:
                     quantise_weight(R_W)
-                s, j = divmod(step - 1, PACK)
-                if j == PACK - 1:
-                    quantise_mix(s)
                 if (step - 1) % 2 == 1 and (step - 1) // 2 < len(LATER_WEIGHTS):
                     quantise_weight(LATER_WEIGHTS[(step - 1) // 2])
             if due(step, UPDATE_LAG):
@@ -293,7 +304,7 @@ def tile_rwkvtimemix_pa_t_kernel(
             if due(step, STATE_OUT_LAG):
                 return_state(*divmod(step - STATE_OUT_LAG, PACK))
             if due(step, GATE_LAG):
-                gate_block(*divmod(step - GATE_LAG, PACK))
+                gate_tile(*divmod(step - GATE_LAG, PACK))
             if due(step, VALUE_LAG):
                 value_block(*divmod(step - VALUE_LAG, PACK))
             if due(step, UPDATE_LAG):

@@ -38,8 +38,9 @@ def block(i):
     return slice(i * P, (i + 1) * P)
 
 
-def runs(a, tiles):
-    return slice(a * P // RUN, (a + tiles) * P // RUN)
+def plane(m):
+    u, e = divmod(m, 2)
+    return slice(2 * u * P + e, 2 * (u + 1) * P, 2)
 
 
 def due(step, lag):
@@ -65,21 +66,28 @@ def tile_rwkvtimemix_pa_t_kernel(
         def load_rows(rows, matrix):
             nc.sync.dma_start(out=rows[:], in_=matrix.rearrange("(a p) c -> p a c", p=P))
 
-        vec_rows = keep.tile([P, P], BF16, name="vec_rows")
+        def load_plane_rows(rows, matrix):
+            nc.sync.dma_start(
+                out=rows[:].rearrange("p (u e) c -> p u e c", u=2),
+                in_=matrix.rearrange("(u p e) c -> p u e c", u=2, e=2),
+            )
+
+        def load_weight(w):
+            (load_rows if w == O_W else load_plane_rows)(w_rows[w], weights[w])
+
+        vec_rows = keep.tile([P, 2 * P], BF16, name="vec_rows")
         nc.vector.memset(vec_rows[:], 0.0)
-        nc.sync.dma_start(out=vec_rows[0:PACK, :], in_=time_decay.rearrange("(j p) -> j p", p=P))
-        nc.sync.dma_start(
-            out=vec_rows[PACK : 2 * PACK, :], in_=time_curve.rearrange("(j p) -> j p", p=P)
-        )
+        nc.sync.dma_start(out=vec_rows[0:2, :], in_=time_decay.rearrange("(u c) -> u c", u=2))
+        nc.sync.dma_start(out=vec_rows[2:4, :], in_=time_curve.rearrange("(u c) -> u c", u=2))
         w_rows = [keep.tile([P, PACK, D], BF16, name="w_rows%d" % w) for w in range(N_WEIGHTS)]
         x_rows = [keep.tile([P, PACK, D], BF16, name="x_rows%d" % s) for s in range(SEQS)]
         state_rows = [keep.tile([P, PACK, D], BF16, name="state_rows%d" % s) for s in range(SEQS)]
         for s in range(SEQS):
             load_rows(x_rows[s], x[s])
             if s == 0:
-                load_rows(w_rows[R_W], weights[R_W])
+                load_weight(R_W)
             if s < len(LATER_WEIGHTS):
-                load_rows(w_rows[LATER_WEIGHTS[s]], weights[LATER_WEIGHTS[s]])
+                load_weight(LATER_WEIGHTS[s])
             else:
                 load_rows(state_rows[s - len(LATER_WEIGHTS)], state[s - len(LATER_WEIGHTS)])
         for s in range(SEQS - len(LATER_WEIGHTS), SEQS):
@@ -103,10 +111,10 @@ def tile_rwkvtimemix_pa_t_kernel(
         for j in range(PACK):
             nc.vector.memset(shifted[j][:, 0:1], 0.0)
 
-        vec_cols = key_bank.tile([P, P], BF16, name="vec_cols", tag="key")
-        nc.tensor.transpose(vec_cols[:], vec_rows[:], ident_bf16[:])
+        vec_cols = key_bank.tile([P, P], F32, name="vec_cols", tag="key")
+        nc.tensor.transpose(vec_cols[:], vec_rows[:].bitcast(F32), ident_f32[:])
         per_channel = keep.tile([P, 2 * PACK], F32, name="per_channel")
-        nc.vector.tensor_copy(out=per_channel[:], in_=vec_cols[:, 0 : 2 * PACK])
+        nc.vector.tensor_copy(out=per_channel[:], in_=vec_cols[:].bitcast(BF16)[:, 0 : 2 * PACK])
         curve = per_channel[:, PACK : 2 * PACK]
         one_minus_curve = keep.tile([P, PACK], F32, name="one_minus_curve")
         nc.vector.tensor_scalar(
@@ -132,19 +140,21 @@ def tile_rwkvtimemix_pa_t_kernel(
 
         def turn_weight(w):
             w_grouped[w] = pairs.tile([P, D, PACK], BF16, name="w_grouped", align_bytes=64)
+            words = w_rows[w][:].bitcast(F32)
+            grouped_words = w_grouped[w][:].bitcast(F32)
             for half in range(2):
-                w_cols = turned_banks.tile([P, 2, PACK, P], BF16, name="w_cols", tag="turned")
+                w_cols = turned_banks.tile([P, 2, 2, P], F32, name="w_cols", tag="turned")
                 for b in range(2):
-                    for j in range(PACK):
+                    for u in range(2):
                         nc.tensor.transpose(
-                            w_cols[:, b, j, :], w_rows[w][:, 2 * half + b, block(j)], ident_bf16[:]
+                            w_cols[:, b, u, :], words[:, 2 * half + b, block(u)], ident_f32[:]
                         )
                 copy = nc.vector.tensor_copy if half == 0 else nc.scalar.copy
                 copy(
-                    out=w_grouped[w][:, 2 * half * P : 2 * (half + 1) * P, :].rearrange(
-                        "p (b o) j -> p b o j", b=2
+                    out=grouped_words[:, 2 * half * P : 2 * (half + 1) * P, :].rearrange(
+                        "p (b o) u -> p b o u", b=2
                     ),
-                    in_=w_cols[:].rearrange("p b j o -> p b o j"),
+                    in_=w_cols[:].rearrange("p b u o -> p b o u"),
                 )
 
         def quantise_weight(w):
@@ -160,7 +170,7 @@ def tile_rwkvtimemix_pa_t_kernel(
             x_cols = scalar_banks.tile([P, T], F32, name="x_cols", tag="scalar")
             for a in range(PACK):
                 nc.tensor.matmul(
-                    x_cols[:, block(a)], lhsT=x_rows[s][:, a, block(j)], rhs=ident_bf16[:],
+                    x_cols[:, block(a)], lhsT=x_rows[s][:, a, plane(j)], rhs=ident_bf16[:],
                     start=True, stop=True,
                 )
             nc.scalar.activation(
@@ -174,12 +184,10 @@ def tile_rwkvtimemix_pa_t_kernel(
 
         def regroup_mix(s):
             xm_grouped[s] = pairs.tile([P, T, PACK], BF16, name="xm_grouped", align_bytes=64)
-            for a in range(PACK):
-                nc.gpsimd.tensor_scalar(
-                    out=xm_grouped[s][:, block(a), :],
-                    in0=xm_planes[s][:, :, block(a)].rearrange("p j t -> p t j"),
-                    scalar1=1.0, scalar2=0.0, op0=ALU.mult, op1=ALU.add,
-                )
+            nc.vector.tensor_copy(
+                out=xm_grouped[s][:].rearrange("p (c i) j -> p c j i", i=RUN),
+                in_=xm_planes[s][:].rearrange("p j (c i) -> p c j i", i=RUN),
+            )
 
         def quantise_mix(s):
             nc.vector.quantize_mx(
@@ -188,53 +196,53 @@ def tile_rwkvtimemix_pa_t_kernel(
                 in_=xm_grouped[s][:].rearrange("p t j -> p (t j)"),
             )
 
-        def product(bank, w, s, m, tokens):
+        def product(bank, w, s, m):
             nc.tensor.matmul_mx(
-                out=bank,
+                out=bank[:],
                 lhsT=w_codes[w][:, block(m)].bitcast(FP8X4),
                 lhsT_scale=w_scales[w][:, block(m)],
-                rhs=xm_codes[:, s, tokens].bitcast(FP8X4),
-                rhs_scale=xm_scales[:, s, tokens],
+                rhs=xm_codes[:, s, :].bitcast(FP8X4),
+                rhs_scale=xm_scales[:, s, :],
                 start=True,
                 stop=True,
             )
 
-        def gate_tile(s, a):
-            if a == 0:
-                gate[s] = triples.tile([P, T // RUN, PACK, RUN], F32, name="gate")
-            r_bank = product_banks.tile([P, PACK, P], F32, name="r_bank", tag="product")
-            for m in range(PACK):
-                product(r_bank[:, m, :], R_W, s, m, block(a))
-            nc.scalar.activation(
-                out=gate[s][:, runs(a, 1), :, :],
-                in_=r_bank[:].rearrange("p m (c i) -> p c m i", i=RUN),
-                func=ACT.Sigmoid,
-            )
+        def gate_block(s, m):
+            if m == 0:
+                gate[s] = triples.tile([P, PACK, T], F32, name="gate")
+            r_bank = product_banks.tile([P, T], F32, name="r_bank", tag="product")
+            product(r_bank, R_W, s, m)
+            nc.scalar.activation(out=gate[s][:, m, :], in_=r_bank[:], func=ACT.Sigmoid)
 
         def value_block(s, m):
             v_bank = product_banks.tile([P, T], F32, name="v_bank", tag="product")
-            product(v_bank[:], V_W, s, m, slice(0, T))
+            product(v_bank, V_W, s, m)
             v_copy[s, m] = quads.tile([P, T], F32, name="v_copy")
             nc.scalar.copy(out=v_copy[s, m][:], in_=v_bank[:])
 
         def turn_state(s, m):
-            state_cols[s, m] = turned_banks.tile([P, T], BF16, name="state_cols", tag="turned")
-            for a in range(PACK):
-                nc.tensor.transpose(
-                    state_cols[s, m][:, block(a)], state_rows[s][:, a, block(m)], ident_bf16[:]
-                )
+            u, e = divmod(m, 2)
+            if e == 0:
+                words = state_rows[s][:].bitcast(F32)
+                state_cols[s, u] = turned_banks.tile([P, T], F32, name="state_cols", tag="turned")
+                for a in range(PACK):
+                    nc.tensor.transpose(
+                        state_cols[s, u][:, block(a)], words[:, a, block(u)], ident_f32[:]
+                    )
 
         def key_times_value(s, m):
             k_bank = key_bank.tile([P, T], F32, name="k_bank", tag="key")
-            product(k_bank[:], K_W, s, m, slice(0, T))
+            product(k_bank, K_W, s, m)
             kv[s, m] = triples.tile([P, T], F32, name="kv")
             nc.vector.tensor_tensor(out=kv[s, m][:], in0=k_bank[:], in1=v_copy[s, m][:], op=ALU.mult)
 
         def update_state(s, m):
             if m == 0:
                 new_state[s] = triples.tile([P, PACK, T], F32, name="new_state")
+            u, e = divmod(m, 2)
+            old = state_cols[s, u][:].bitcast(BF16).rearrange("p (t e) -> p e t", e=2)[:, e, :]
             nc.vector.scalar_tensor_tensor(
-                out=new_state[s][:, m, :], in0=state_cols[s, m][:], scalar=decay[:, m : m + 1],
+                out=new_state[s][:, m, :], in0=old, scalar=decay[:, m : m + 1],
                 in1=kv[s, m][:], op0=ALU.mult, op1=ALU.add,
             )
 
@@ -243,7 +251,7 @@ def tile_rwkvtimemix_pa_t_kernel(
             tokens = slice(a * P, (a + TILES) * P)
             nc.vector.tensor_tensor(
                 out=h_grouped[s, a][:].rearrange("p (c i) m -> p c m i", i=RUN),
-                in0=gate[s][:, runs(a, TILES), :, :],
+                in0=gate[s][:, :, tokens].rearrange("p m (c i) -> p c m i", i=RUN),
                 in1=new_state[s][:, :, tokens].rearrange("p m (c i) -> p c m i", i=RUN),
                 op=ALU.mult,
             )
@@ -264,7 +272,10 @@ def tile_rwkvtimemix_pa_t_kernel(
                     state_bank[:, block(m)], new_state[s][:, m, block(a)], ident_f32[:]
                 )
             state_out = quads.tile([P, D], F32, name="state_out")
-            nc.scalar.copy(out=state_out[:], in_=state_bank[:])
+            nc.scalar.copy(
+                out=state_out[:].rearrange("t (u p e) -> t u p e", u=2, e=2),
+                in_=state_bank[:].rearrange("t (u e p) -> t u p e", u=2, e=2),
+            )
             nc.sync.dma_start(out=out_1[s, block(a), :], in_=state_out[:])
 
         def project(s, a):
@@ -292,8 +303,8 @@ def tile_rwkvtimemix_pa_t_kernel(
                     turn_weight(LATER_WEIGHTS[step // 2])
                 if step == 0:
                     turn_weight(R_W)
-            if due(step, 2) and (step - 2) % PACK == PACK - 1:
-                quantise_mix((step - 2) // PACK)
+            if due(step, 1) and (step - 1) % PACK == PACK - 1:
+                quantise_mix((step - 1) // PACK)
             if due(step, 1):
                 if step == 1:
                     quantise_weight(R_W)
@@ -304,7 +315,7 @@ def tile_rwkvtimemix_pa_t_kernel(
             if due(step, STATE_OUT_LAG):
                 return_state(*divmod(step - STATE_OUT_LAG, PACK))
             if due(step, GATE_LAG):
-                gate_tile(*divmod(step - GATE_LAG, PACK))
+                gate_block(*divmod(step - GATE_LAG, PACK))
             if due(step, VALUE_LAG):
                 value_block(*divmod(step - VALUE_LAG, PACK))
             if due(step, UPDATE_LAG):

@@ -185,8 +185,8 @@ def tile_rwkvtimemix_pa_t_kernel(
         def regroup_mix(s):
             xm_grouped[s] = pairs.tile([P, T, PACK], BF16, name="xm_grouped", align_bytes=64)
             nc.vector.tensor_copy(
-                out=xm_grouped[s][:].rearrange("p (c i) j -> p c j i", i=RUN),
-                in_=xm_planes[s][:].rearrange("p j (c i) -> p c j i", i=RUN),
+                out=xm_grouped[s][:].rearrange("p (c i) j -> p c j i", i=2 * RUN),
+                in_=xm_planes[s][:].rearrange("p j (c i) -> p c j i", i=2 * RUN),
             )
 
         def quantise_mix(s):
@@ -209,10 +209,13 @@ def tile_rwkvtimemix_pa_t_kernel(
 
         def gate_block(s, m):
             if m == 0:
-                gate[s] = triples.tile([P, PACK, T], F32, name="gate")
+                gate[s] = triples.tile([P, T // RUN, PACK, RUN], F32, name="gate")
             r_bank = product_banks.tile([P, T], F32, name="r_bank", tag="product")
             product(r_bank, R_W, s, m)
-            nc.scalar.activation(out=gate[s][:, m, :], in_=r_bank[:], func=ACT.Sigmoid)
+            nc.scalar.activation(
+                out=gate[s][:, :, m, :], in_=r_bank[:].rearrange("p (c i) -> p c i", i=RUN),
+                func=ACT.Sigmoid,
+            )
 
         def value_block(s, m):
             v_bank = product_banks.tile([P, T], F32, name="v_bank", tag="product")
@@ -251,7 +254,7 @@ def tile_rwkvtimemix_pa_t_kernel(
             tokens = slice(a * P, (a + TILES) * P)
             nc.vector.tensor_tensor(
                 out=h_grouped[s, a][:].rearrange("p (c i) m -> p c m i", i=RUN),
-                in0=gate[s][:, :, tokens].rearrange("p m (c i) -> p c m i", i=RUN),
+                in0=gate[s][:, a * P // RUN : (a + TILES) * P // RUN, :, :],
                 in1=new_state[s][:, :, tokens].rearrange("p m (c i) -> p c m i", i=RUN),
                 op=ALU.mult,
             )

from contextlib import ExitStack

import concourse.mybir as mybir
from concourse.masks import make_identity

F32 = mybir.dt.float32
BF16 = mybir.dt.bfloat16
U32 = mybir.dt.uint32
U8 = mybir.dt.uint8
FP8X4 = mybir.dt.float8_e4m3fn_x4
ACT = mybir.ActivationFunctionType
ALU = mybir.AluOpType

P = 128
PACK = 4
SEQS = 8
T = 512
D = 512
N_WEIGHTS = 4
K_W, V_W, R_W, O_W = 0, 1, 2, 3
LATER_WEIGHTS = (V_W, K_W, O_W)

FLOPS = 2 * N_WEIGHTS * SEQS * T * D * D

STEPS = SEQS * PACK
RUN = 4
TILES = 2
GATE_LAG = PACK + 2
VALUE_LAG = PACK + 3
UPDATE_LAG = PACK + 4
HIDDEN_LAG = UPDATE_LAG + PACK
QUANTISE_LAG = HIDDEN_LAG + 1
STATE_OUT_LAG = UPDATE_LAG + PACK + 1
PROJECT_LAG = QUANTISE_LAG + 2


def block(i):
    return slice(i * P, (i + 1) * P)


def plane(m):
    u, e = divmod(m, 2)
    return slice(2 * u * P + e, 2 * (u + 1) * P, 2)


def due(step, lag):
    return 0 <= step - lag < STEPS


def tile_rwkvtimemix_pa_t_kernel(
    tc, x, state, Wk, Wv, Wr, Wo, time_decay, time_curve, out_0, out_1
):
    nc = tc.nc
    weights = (Wk, Wv, Wr, Wo)

    with ExitStack() as stack:
        keep = stack.enter_context(tc.tile_pool(name="keep", bufs=1))
        pairs = stack.enter_context(tc.tile_pool(name="pairs", bufs=2))
        triples = stack.enter_context(tc.tile_pool(name="triples", bufs=3))
        quads = stack.enter_context(tc.tile_pool(name="quads", bufs=4))
        scalar_banks = stack.enter_context(tc.psum_pool(name="scalar_banks", bufs=3))
        product_banks = stack.enter_context(tc.psum_pool(name="product_banks", bufs=2))
        turned_banks = stack.enter_context(tc.psum_pool(name="turned_banks", bufs=2))
        key_bank = stack.enter_context(tc.psum_pool(name="key_bank", bufs=1))

        def load_rows(rows, matrix):
            nc.sync.dma_start(out=rows[:], in_=matrix.rearrange("(a p) c -> p a c", p=P))

        def load_plane_rows(rows, matrix):
            nc.sync.dma_start(
                out=rows[:].rearrange("p (u e) c -> p u e c", u=2),
                in_=matrix.rearrange("(u p e) c -> p u e c", u=2, e=2),
            )

        def load_weight(w):
            (load_rows if w == O_W else load_plane_rows)(w_rows[w], weights[w])

        vec_rows = keep.tile([P, 2 * P], BF16, name="vec_rows")
        nc.vector.memset(vec_rows[:], 0.0)
        nc.sync.dma_start(out=vec_rows[0:2, :], in_=time_decay.rearrange("(u c) -> u c", u=2))
        nc.sync.dma_start(out=vec_rows[2:4, :], in_=time_curve.rearrange("(u c) -> u c", u=2))
        w_rows = [keep.tile([P, PACK, D], BF16, name="w_rows%d" % w) for w in range(N_WEIGHTS)]
        x_rows = [keep.tile([P, PACK, D], BF16, name="x_rows%d" % s) for s in range(SEQS)]
        state_rows = [keep.tile([P, PACK, D], BF16, name="state_rows%d" % s) for s in range(SEQS)]
        for s in range(SEQS):
            load_rows(x_rows[s], x[s])
            if s == 0:
                load_weight(R_W)
            if s < len(LATER_WEIGHTS):
                load_weight(LATER_WEIGHTS[s])
            else:
                load_rows(state_rows[s - len(LATER_WEIGHTS)], state[s - len(LATER_WEIGHTS)])
        for s in range(SEQS - len(LATER_WEIGHTS), SEQS):
            load_rows(state_rows[s], state[s])

        ident_bf16 = keep.tile([P, P], BF16, name="ident_bf16")
        make_identity(nc, ident_bf16[:])
        ident_f32 = keep.tile([P, P], F32, name="ident_f32")
        make_identity(nc, ident_f32[:])

        w_codes = [
            keep.tile([P, D], U32, name="w_codes%d" % w, align_bytes=64) for w in range(N_WEIGHTS)
        ]
        w_scales = [
            keep.tile([P, D], U8, name="w_scales%d" % w, align_bytes=64) for w in range(N_WEIGHTS)
        ]
        xm_codes = keep.tile([P, SEQS, T], U32, name="xm_codes", align_bytes=64)
        xm_scales = keep.tile([P, SEQS, T], U8, name="xm_scales", align_bytes=64)

        shifted = [keep.tile([P, T], F32, name="shifted%d" % j) for j in range(PACK)]
        for j in range(PACK):
            nc.vector.memset(shifted[j][:, 0:1], 0.0)

        vec_cols = key_bank.tile([P, P], F32, name="vec_cols", tag="key")
        nc.tensor.transpose(vec_cols[:], vec_rows[:].bitcast(F32), ident_f32[:])
        per_channel = keep.tile([P, 2 * PACK], F32, name="per_channel")
        nc.vector.tensor_copy(out=per_channel[:], in_=vec_cols[:].bitcast(BF16)[:, 0 : 2 * PACK])
        curve = per_channel[:, PACK : 2 * PACK]
        one_minus_curve = keep.tile([P, PACK], F32, name="one_minus_curve")
        nc.vector.tensor_scalar(
            out=one_minus_curve[:], in0=curve, scalar1=-1.0, scalar2=1.0,
            op0=ALU.mult, op1=ALU.add,
        )
        rate = keep.tile([P, PACK], F32, name="rate")
        nc.scalar.activation(out=rate[:], in_=per_channel[:, 0:PACK], func=ACT.Exp)
        decay = keep.tile([P, PACK], F32, name="decay")
        nc.scalar.activation(out=decay[:], in_=rate[:], func=ACT.Exp, scale=-1.0)

        w_grouped = {}
        xm_planes = {}
        xm_grouped = {}
        gate = {}
        v_copy = {}
        kv = {}
        state_cols = {}
        new_state = {}
        h_grouped = {}
        h_codes = {}
        h_scales = {}

        def turn_weight(w):
            w_grouped[w] = pairs.tile([P, D, PACK], BF16, name="w_grouped", align_bytes=64)
            words = w_rows[w][:].bitcast(F32)
            grouped_words = w_grouped[w][:].bitcast(F32)
            for half in range(2):
                w_cols = turned_banks.tile([P, 2, 2, P], F32, name="w_cols", tag="turned")
                for b in range(2):
                    for u in range(2):
                        nc.tensor.transpose(
                            w_cols[:, b, u, :], words[:, 2 * half + b, block(u)], ident_f32[:]
                        )
                copy = nc.vector.tensor_copy if half == 0 else nc.scalar.copy
                copy(
                    out=grouped_words[:, 2 * half * P : 2 * (half + 1) * P, :].rearrange(
                        "p (b o) u -> p b o u", b=2
                    ),
                    in_=w_cols[:].rearrange("p b u o -> p b o u"),
                )

        def quantise_weight(w):
            nc.vector.quantize_mx(
                out=w_codes[w][:].bitcast(FP8X4),
                scales=w_scales[w][:],
                in_=w_grouped[w][:].rearrange("p o j -> p (o j)"),
            )

        def mix_plane(s, j):
            if j == 0:
                xm_planes[s] = pairs.tile([P, PACK, T], BF16, name="xm_planes")
            x_cols = scalar_banks.tile([P, T], F32, name="x_cols", tag="scalar")
            for a in range(PACK):
                nc.tensor.matmul(
                    x_cols[:, block(a)], lhsT=x_rows[s][:, a, plane(j)], rhs=ident_bf16[:],
                    start=True, stop=True,
                )
            nc.scalar.activation(
                out=shifted[j][:, 1:T], in_=x_cols[:, 0 : T - 1], func=ACT.Copy,
                scale=one_minus_curve[:, j : j + 1],
            )
            nc.vector.scalar_tensor_tensor(
                out=xm_planes[s][:, j, :], in0=x_cols[:], scalar=curve[:, j : j + 1],
                in1=shifted[j][:], op0=ALU.mult, op1=ALU.add,
            )

        def regroup_mix(s):
            xm_grouped[s] = pairs.tile([P, T, PACK], BF16, name="xm_grouped", align_bytes=64)
            nc.vector.tensor_copy(
                out=xm_grouped[s][:].rearrange("p (c i) j -> p c j i", i=2 * RUN),
                in_=xm_planes[s][:].rearrange("p j (c i) -> p c j i", i=2 * RUN),
            )

        def quantise_mix(s):
            nc.vector.quantize_mx(
                out=xm_codes[:, s, :].bitcast(FP8X4),
                scales=xm_scales[:, s, :],
                in_=xm_grouped[s][:].rearrange("p t j -> p (t j)"),
            )

        def product(bank, w, s, m):
            nc.tensor.matmul_mx(
                out=bank[:],
                lhsT=w_codes[w][:, block(m)].bitcast(FP8X4),
                lhsT_scale=w_scales[w][:, block(m)],
                rhs=xm_codes[:, s, :].bitcast(FP8X4),
                rhs_scale=xm_scales[:, s, :],
                start=True,
                stop=True,
            )

        def gate_block(s, m):
            if m == 0:
                gate[s] = triples.tile([P, T // RUN, PACK, RUN], F32, name="gate")
            r_bank = product_banks.tile([P, T], F32, name="r_bank", tag="product")
            product(r_bank, R_W, s, m)
            nc.scalar.activation(
                out=gate[s][:, :, m, :], in_=r_bank[:].rearrange("p (c i) -> p c i", i=RUN),
                func=ACT.Sigmoid,
            )

        def value_block(s, m):
            v_bank = product_banks.tile([P, T], F32, name="v_bank", tag="product")
            product(v_bank, V_W, s, m)
            v_copy[s, m] = quads.tile([P, T], F32, name="v_copy")
            nc.scalar.copy(out=v_copy[s, m][:], in_=v_bank[:])

        def turn_state(s, m):
            u, e = divmod(m, 2)
            if e == 0:
                words = state_rows[s][:].bitcast(F32)
                state_cols[s, u] = turned_banks.tile([P, T], F32, name="state_cols", tag="turned")
                for a in range(PACK):
                    nc.tensor.transpose(
                        state_cols[s, u][:, block(a)], words[:, a, block(u)], ident_f32[:]
                    )

        def key_times_value(s, m):
            k_bank = key_bank.tile([P, T], F32, name="k_bank", tag="key")
            product(k_bank, K_W, s, m)
            kv[s, m] = triples.tile([P, T], F32, name="kv")
            nc.vector.tensor_tensor(out=kv[s, m][:], in0=k_bank[:], in1=v_copy[s, m][:], op=ALU.mult)

        def update_state(s, m):
            if m == 0:
                new_state[s] = triples.tile([P, PACK, T], F32, name="new_state")
            u, e = divmod(m, 2)
            old = state_cols[s, u][:].bitcast(BF16).rearrange("p (t e) -> p e t", e=2)[:, e, :]
            nc.vector.scalar_tensor_tensor(
                out=new_state[s][:, m, :], in0=old, scalar=decay[:, m : m + 1],
                in1=kv[s, m][:], op0=ALU.mult, op1=ALU.add,
            )

        def hidden(s, a):
            h_grouped[s, a] = triples.tile([P, TILES * P, PACK], BF16, name="h_grouped", align_bytes=64)
            tokens = slice(a * P, (a + TILES) * P)
            nc.vector.tensor_tensor(
                out=h_grouped[s, a][:].rearrange("p (c i) m -> p c m i", i=RUN),
                in0=gate[s][:, a * P // RUN : (a + TILES) * P // RUN, :, :],
                in1=new_state[s][:, :, tokens].rearrange("p m (c i) -> p c m i", i=RUN),
                op=ALU.mult,
            )

        def quantise_hidden(s, a):
            h_codes[s, a] = triples.tile([P, TILES * P], U32, name="h_codes", align_bytes=64)
            h_scales[s, a] = triples.tile([P, TILES * P], U8, name="h_scales", align_bytes=64)
            nc.vector.quantize_mx(
                out=h_codes[s, a][:].bitcast(FP8X4),
                scales=h_scales[s, a][:],
                in_=h_grouped[s, a][:].rearrange("p t m -> p (t m)"),
            )

        def return_state(s, a):
            state_bank = scalar_banks.tile([P, D], F32, name="state_bank", tag="scalar")
            for m in range(PACK):
                nc.tensor.transpose(
                    state_bank[:, block(m)], new_state[s][:, m, block(a)], ident_f32[:]
                )
            state_out = quads.tile([P, D], F32, name="state_out")
            nc.scalar.copy(
                out=state_out[:].rearrange("t (u p e) -> t u p e", u=2, e=2),
                in_=state_bank[:].rearrange("t (u e p) -> t u p e", u=2, e=2),
            )
            nc.sync.dma_start(out=out_1[s, block(a), :], in_=state_out[:])

        def project(s, a):
            out_bank = scalar_banks.tile([P, D], F32, name="out_bank", tag="scalar")
            nc.tensor.matmul_mx(
                out=out_bank[:],
                lhsT=h_codes[s, a - a % TILES][:, block(a % TILES)].bitcast(FP8X4),
                lhsT_scale=h_scales[s, a - a % TILES][:, block(a % TILES)],
                rhs=w_codes[O_W][:].bitcast(FP8X4),
                rhs_scale=w_scales[O_W][:],
                start=True,
                stop=True,
            )
            out_rows = quads.tile([P, D], F32, name="out_rows")
            nc.scalar.copy(out=out_rows[:], in_=out_bank[:])
            nc.sync.dma_start(out=out_0[s, block(a), :], in_=out_rows[:])

        for step in range(STEPS + PROJECT_LAG):
            if due(step, 0):
                s, j = divmod(step, PACK)
                mix_plane(s, j)
                if j == PACK - 1:
                    regroup_mix(s)
                if step % 2 == 1 and step // 2 < len(LATER_WEIGHTS):
                    turn_weight(LATER_WEIGHTS[step // 2])
                if step == 0:
                    turn_weight(R_W)
            if due(step, 1) and (step - 1) % PACK == PACK - 1:
                quantise_mix((step - 1) // PACK)
            if due(step, 1):
                if step == 1:
                    quantise_weight(R_W)
                if (step - 1) % 2 == 1 and (step - 1) // 2 < len(LATER_WEIGHTS):
                    quantise_weight(LATER_WEIGHTS[(step - 1) // 2])
            if due(step, UPDATE_LAG):
                turn_state(*divmod(step - UPDATE_LAG, PACK))
            if due(step, STATE_OUT_LAG):
                return_state(*divmod(step - STATE_OUT_LAG, PACK))
            if due(step, GATE_LAG):
                gate_block(*divmod(step - GATE_LAG, PACK))
            if due(step, VALUE_LAG):
                value_block(*divmod(step - VALUE_LAG, PACK))
            if due(step, UPDATE_LAG):
                key_times_value(*divmod(step - UPDATE_LAG, PACK))
            if due(step, HIDDEN_LAG) and (step - HIDDEN_LAG) % TILES == 0:
                hidden(*divmod(step - HIDDEN_LAG, PACK))
            if due(step, UPDATE_LAG):
                update_state(*divmod(step - UPDATE_LAG, PACK))
            if due(step, QUANTISE_LAG) and (step - QUANTISE_LAG) % TILES == 0:
                quantise_hidden(*divmod(step - QUANTISE_LAG, PACK))
            if due(step, PROJECT_LAG):
                project(*divmod(step - PROJECT_LAG, PACK))
